import numpy as np
import ml_dtypes


def mxq(x, axis, fmt="e4m3"):
    dtype, down = {"e4m3": (ml_dtypes.float8_e4m3fn, 7), "e5m2": (ml_dtypes.float8_e5m2, 14)}[fmt]
    v = np.moveaxis(np.asarray(x, np.float32).astype(ml_dtypes.bfloat16).astype(np.float64), axis, -1)
    blocks = v.reshape(v.shape[:-1] + (-1, 32))
    amax = np.abs(blocks).max(-1, keepdims=True)
    byte = np.maximum(np.where(amax > 0, np.frexp(amax)[1] - 1 + 127, 0) - down, 1)
    scale = np.exp2(byte - 127.0)
    codes = (blocks / scale).astype(np.float32).astype(dtype).astype(np.float64)
    return np.moveaxis((codes * scale).reshape(v.shape), -1, axis)


WIDE = False


def mx_kscale(k):
    if not WIDE:
        return np.ones(k)
    levels = np.array([10, -10, 5, -5, 0])
    a = np.random.permutation(np.resize(levels, k // 512 * 4)).reshape(k // 512, 4)
    idx = np.arange(k)
    return np.exp2(a[idx // 512, idx % 128 // 32])


BF16 = ml_dtypes.bfloat16


def bf(x):
    return np.asarray(x, np.float32).astype(BF16)


def f64(x):
    return np.asarray(x).astype(np.float64)


B, STOCH, ACT_DIM, HIDDEN, DETER = 256, 1024, 512, 2048, 2048
EPS = 1e-4
DT_MIN = 1e-4


def softplus(v):
    return np.maximum(v, 0.0) + np.log1p(np.exp(-np.abs(v)))


def sigmoid(v):
    return 1.0 / (1.0 + np.exp(-v))


def rmsnorm(v, w):
    return v * (1.0 / np.sqrt(np.mean(v * v, axis=-1, keepdims=True) + EPS)) * w


def setup_inputs():
    s = mx_kscale(DETER)
    r = np.maximum(s, 1.0)

    def w():
        return np.random.standard_normal((DETER, DETER)) / np.sqrt(DETER) / s

    def bias():
        return np.random.standard_normal(DETER) * 0.2

    return {"x": bf(np.random.standard_normal((B, DETER)) * 0.9 * s),
            "deter": bf(np.random.standard_normal((B, DETER))),
            "a_base": bf(np.random.standard_normal(DETER)),
            "dt_w": bf(w()), "dt_b": bf(bias()),
            "b_w": bf(w()), "b_b": bf(bias()),
            "c_w": bf(w() / r[:, None]), "c_b": bf(bias() / r),
            "z_w": bf(w()), "z_b": bf(bias()),
            "skip": bf(np.random.standard_normal(DETER) * 0.5 / s),
            "norm_w": bf(1.0 + 0.1 * np.random.standard_normal(DETER))}


def reference(x, deter, a_base, dt_w, dt_b, b_w, b_b, c_w, c_b, z_w, z_b, skip, norm_w):
    x, deter = f64(x), f64(deter)
    xq = mxq(x, 1, "e4m3")
    dt = softplus((xq @ mxq(f64(dt_w), 1, "e4m3").T) + f64(dt_b)) + DT_MIN
    a = -softplus(f64(a_base))
    b = np.tanh((xq @ mxq(f64(b_w), 1, "e4m3").T) + f64(b_b))
    c = (xq @ mxq(f64(c_w), 1, "e4m3").T) + f64(c_b)
    z = sigmoid((xq @ mxq(f64(z_w), 1, "e4m3").T) + f64(z_b))
    state = np.exp(a * dt) * deter + dt * b * x
    y = c * state + f64(skip) * x
    out = z * y + (1.0 - z) * deter
    return rmsnorm(out, f64(norm_w))

@@ -1,0 +1,474 @@
+from contextlib import ExitStack
+
+import concourse.mybir as mybir
+from concourse.masks import make_identity
+
+F32 = mybir.dt.float32
+BF16 = mybir.dt.bfloat16
+U32 = mybir.dt.uint32
+U8 = mybir.dt.uint8
+FP8X4 = mybir.dt.float8_e4m3fn_x4
+ACT = mybir.ActivationFunctionType
+ALU = mybir.AluOpType
+
+P = 128
+TOKENS = 256
+CHANNELS = 2048
+PAIR = 2
+PACK = 4
+PASSES = CHANNELS // (P * PACK)
+GROUP_ROWS = PAIR * P
+GROUPS = CHANNELS // GROUP_ROWS
+GROUP_COLS = PAIR * TOKENS
+ROW_WORDS = CHANNELS // PAIR
+BANK = 512
+BANKS_PER_GROUP = PAIR * ROW_WORDS // BANK
+
+GATES = ["dt", "c", "b", "z"]
+LOADS_AHEAD = 3
+EPS = 1e-4
+DT_MIN = 1e-4
+EXP_CAP = 20.0
+
+A_BASE = 0
+DT_B = 1
+B_B = 2
+C_B = 3
+Z_B = 4
+SKIP = 5
+NORM_W = 6
+
+FLOPS = 4 * 2 * TOKENS * CHANNELS * CHANNELS
+
+
+def tile_mamba2backbone_pb_kernel(
+    tc, x, deter, a_base, dt_w, dt_b, b_w, b_b, c_w, c_b, z_w, z_b, skip, norm_w, out
+):
+    nc = tc.nc
+    weights = {"dt": dt_w, "c": c_w, "b": b_w, "z": z_w}
+    vectors = [a_base, dt_b, b_b, c_b, z_b, skip, norm_w]
+
+    with ExitStack() as stack:
+        const = stack.enter_context(tc.tile_pool(name="const", bufs=1))
+        keep = stack.enter_context(tc.tile_pool(name="keep", bufs=1))
+        raw_pool = stack.enter_context(tc.tile_pool(name="raw", bufs=LOADS_AHEAD + 2))
+        grouped_pool = stack.enter_context(tc.tile_pool(name="grouped", bufs=3))
+        mx_pool = stack.enter_context(tc.tile_pool(name="mx", bufs=2))
+        temp = stack.enter_context(tc.tile_pool(name="temp", bufs=3))
+        store_pool = stack.enter_context(tc.tile_pool(name="store", bufs=4))
+        flip_psum = stack.enter_context(tc.psum_pool(name="flip", bufs=5))
+        sum_psum = stack.enter_context(tc.psum_pool(name="sums", bufs=2))
+        stack.enter_context(tc.manual_schedule())
+
+        ident = const.tile([P, P], F32)
+        make_identity(nc, ident[:])
+        one_col = const.tile([P, 1], F32)
+        nc.vector.memset(one_col[:], 1.0)
+        eps_col = const.tile([P, 1], F32)
+        nc.vector.memset(eps_col[:], EPS)
+        sqrt_warm = const.tile([P, 1], F32)
+        ones = const.tile([P, 32], F32)
+        nc.vector.memset(ones[:], 1.0)
+        square_sum = keep.tile([P, GROUP_COLS], F32)
+        nc.vector.memset(square_sum[:], 0.0)
+
+        def load_rows(rows_view):
+            rows = raw_pool.tile([P, PAIR * CHANNELS], BF16, tag="raw")
+            nc.sync.dma_start(out=rows[:].rearrange("p (r k) -> p r k", r=PAIR), in_=rows_view)
+            return rows
+
+        raw = {}
+
+        def load_group(index):
+            gate, j = GATES[index // GROUPS], index % GROUPS
+            rows = weights[gate][GROUP_ROWS * j : GROUP_ROWS * (j + 1), :]
+            raw[index] = load_rows(rows.rearrange("(p e) k -> p e k", e=PAIR))
+
+        x_rows = load_rows(x.rearrange("(t p) k -> p t k", p=P))
+        vector_rows = const.tile([P, GROUP_ROWS], BF16)
+        nc.vector.memset(vector_rows[:], 0.0)
+        for i, vector in enumerate(vectors):
+            nc.scalar.dma_start(
+                out=vector_rows[GROUPS * i : GROUPS * (i + 1), :],
+                in_=vector.rearrange("(j c) -> j c", j=GROUPS),
+            )
+        load_group(0)
+        load_group(1)
+        deter_rows = load_rows(deter.rearrange("(t p) k -> p t k", p=P))
+        load_group(2)
+
+        def empty_bank(position, out_words, bank_view):
+            if position % BANKS_PER_GROUP == 0:
+                nc.vector.tensor_copy(out=out_words, in_=bank_view)
+            else:
+                nc.scalar.copy(out=out_words, in_=bank_view)
+
+        def transpose_tokens(rows, name):
+            words = rows[:].bitcast(F32)
+            tiles = []
+            for g in range(PASSES):
+                bank = flip_psum.tile([P, BANK], F32, tag="flip")
+                for u in range(PAIR):
+                    for t in range(TOKENS // P):
+                        first_word = ROW_WORDS * t + P * (PAIR * g + u)
+                        nc.tensor.transpose(
+                            bank[:, TOKENS * u + P * t : TOKENS * u + P * (t + 1)],
+                            words[:, first_word : first_word + P],
+                            ident[:],
+                        )
+                by_k = keep.tile([P, TOKENS * PACK], BF16, name="%s%d" % (name, g), align_bytes=64)
+                empty_bank(
+                    g,
+                    by_k[:].bitcast(F32).rearrange("p (t u) -> p t u", u=PAIR),
+                    bank[:].rearrange("p (u t) -> p t u", u=PAIR),
+                )
+                tiles.append(by_k)
+            return tiles
+
+        def group_view(tiles, j):
+            g, u = j // PAIR, j % PAIR
+            return tiles[g][:].rearrange("p (t c) -> p c t", c=PACK)[:, PAIR * u : PAIR * (u + 1), :]
+
+        x_by_k = transpose_tokens(x_rows, "x")
+        x_codes = keep.tile([P, PASSES * TOKENS], U32, align_bytes=64)
+        x_scales = keep.tile([P, PASSES * TOKENS], U8, align_bytes=64)
+        for g in range(PASSES):
+            cols = slice(TOKENS * g, TOKENS * (g + 1))
+            nc.vector.quantize_mx(
+                out=x_codes[:, cols].bitcast(FP8X4), scales=x_scales[:, cols], in_=x_by_k[g][:]
+            )
+
+        vector_bank = flip_psum.tile([P, BANK], F32, tag="flip")
+        nc.tensor.transpose(vector_bank[:, 0:P], vector_rows[:].bitcast(F32), ident[:])
+        table = const.tile([P, PAIR * P], F32)
+        nc.vector.tensor_copy(out=table[:], in_=vector_bank[:, 0:P].bitcast(BF16))
+
+        def rows_of(which):
+            return table[:, PAIR * GROUPS * which : PAIR * GROUPS * (which + 1)]
+
+        def scalar_of(columns, j, e):
+            return columns[:, PAIR * j + e : PAIR * j + e + 1]
+
+        z_b_half = const.tile([P, PAIR * GROUPS], F32)
+        nc.vector.tensor_scalar_mul(out=z_b_half[:], in0=rows_of(Z_B), scalar1=0.5)
+        a_work = const.tile([P, PAIR * GROUPS], F32)
+        nc.vector.tensor_scalar_min(out=a_work[:], in0=rows_of(A_BASE), scalar1=EXP_CAP)
+        nc.scalar.activation(out=a_work[:], in_=a_work[:], func=ACT.Exp)
+        a_neg = const.tile([P, PAIR * GROUPS], F32)
+        a_neg_dt_min = const.tile([P, PAIR * GROUPS], F32)
+
+        def group_tiles(name):
+            return [keep.tile([P, GROUP_COLS], F32, name="%s%d" % (name, j)) for j in range(GROUPS)]
+
+        def halves(group_tile):
+            return group_tile[:].rearrange("p (e t) -> p e t", e=PAIR)
+
+        soft = group_tiles("soft")
+        decay = group_tiles("decay")
+        state = group_tiles("state")
+        c_gate = group_tiles("cgate")
+        mix = group_tiles("mix")
+
+        banks = {}
+        grouped = {}
+        codes = {}
+        scales = {}
+        sums = {}
+
+        def transpose_group(index):
+            words = raw[index][:].bitcast(F32)
+            banks[index] = []
+            for b in range(BANKS_PER_GROUP):
+                bank = flip_psum.tile([P, BANK], F32, tag="flip")
+                for piece in range(BANK // P):
+                    first_word = BANK * b + P * piece
+                    nc.tensor.transpose(
+                        bank[:, P * piece : P * (piece + 1)],
+                        words[:, first_word : first_word + P],
+                        ident[:],
+                    )
+                banks[index].append(bank)
+            grouped[index] = grouped_pool.tile(
+                [P, PAIR * CHANNELS], BF16, name="grouped", tag="grouped", align_bytes=64
+            )
+
+        def empty_group_bank(index, b):
+            empty_bank(
+                b,
+                grouped[index][:]
+                .bitcast(F32)[:, BANK * b : BANK * (b + 1)]
+                .rearrange("p (g n u) -> p g n u", g=PAIR, u=PAIR),
+                banks[index][b][:].rearrange("p (g u n) -> p g n u", g=PAIR, u=PAIR),
+            )
+
+        def quantise_group(index):
+            codes[index] = mx_pool.tile(
+                [P, PAIR * PASSES * P], U32, name="codes", tag="codes", align_bytes=64
+            )
+            scales[index] = mx_pool.tile(
+                [P, PAIR * PASSES * P], U8, name="scales", tag="scales", align_bytes=64
+            )
+            nc.vector.quantize_mx(
+                out=codes[index][:].bitcast(FP8X4), scales=scales[index][:], in_=grouped[index][:]
+            )
+
+        def multiply_group(index):
+            sums[index] = sum_psum.tile([P, GROUP_COLS], F32, name="sums", tag="sums")
+            for e in range(PAIR):
+                for g in range(PASSES):
+                    w_cols = slice(P * (PASSES * e + g), P * (PASSES * e + g + 1))
+                    x_cols = slice(TOKENS * g, TOKENS * (g + 1))
+                    nc.tensor.matmul_mx(
+                        out=sums[index][:, TOKENS * e : TOKENS * (e + 1)],
+                        lhsT=codes[index][:, w_cols].bitcast(FP8X4),
+                        lhsT_scale=scales[index][:, w_cols],
+                        rhs=x_codes[:, x_cols].bitcast(FP8X4),
+                        rhs_scale=x_scales[:, x_cols],
+                        start=(g == 0),
+                        stop=(g == PASSES - 1),
+                    )
+
+        def activate_sums(gate, j, out_tile, func, bias_columns, scale):
+            for e in range(PAIR):
+                cols = slice(TOKENS * e, TOKENS * (e + 1))
+                nc.scalar.activation(
+                    out=out_tile[:, cols],
+                    in_=sums[GROUPS * GATES.index(gate) + j][:, cols],
+                    func=func,
+                    bias=scalar_of(bias_columns, j, e),
+                    scale=scale,
+                )
+
+        def dt_argument(j):
+            activate_sums("dt", j, soft[j], ACT.Identity, rows_of(DT_B), 1.0)
+
+        def dt_cap(j):
+            nc.vector.tensor_scalar_min(out=decay[j][:], in0=soft[j][:], scalar1=EXP_CAP)
+
+        def dt_exp(j):
+            nc.scalar.activation(out=decay[j][:], in_=decay[j][:], func=ACT.Exp)
+
+        def dt_log(j):
+            nc.scalar.activation(out=decay[j][:], in_=decay[j][:], func=ACT.Ln, bias=one_col[:])
+
+        def dt_softplus(j):
+            nc.vector.tensor_tensor(out=soft[j][:], in0=soft[j][:], in1=decay[j][:], op=ALU.max)
+
+        def skip_minus_deter(j):
+            for e in range(PAIR):
+                nc.vector.scalar_tensor_tensor(
+                    out=halves(mix[j])[:, e, :],
+                    in0=group_view(x_by_k, j)[:, e, :],
+                    scalar=scalar_of(rows_of(SKIP), j, e),
+                    in1=group_view(deter_by_k, j)[:, e, :],
+                    op0=ALU.mult,
+                    op1=ALU.subtract,
+                )
+
+        def dt_times_x(j):
+            nc.vector.scalar_tensor_tensor(
+                out=halves(state[j]),
+                in0=halves(soft[j]),
+                scalar=DT_MIN,
+                in1=group_view(x_by_k, j),
+                op0=ALU.add,
+                op1=ALU.mult,
+            )
+
+        def decay_exp(j):
+            for e in range(PAIR):
+                cols = slice(TOKENS * e, TOKENS * (e + 1))
+                nc.scalar.activation(
+                    out=decay[j][:, cols],
+                    in_=soft[j][:, cols],
+                    func=ACT.Exp,
+                    bias=scalar_of(a_neg_dt_min, j, e),
+                    scale=scalar_of(a_neg, j, e),
+                )
+
+        def decay_times_deter(j):
+            nc.gpsimd.tensor_tensor(
+                out=halves(decay[j]),
+                in0=halves(decay[j]),
+                in1=group_view(deter_by_k, j),
+                op=ALU.mult,
+            )
+
+        def c_argument(j):
+            activate_sums("c", j, c_gate[j], ACT.Identity, rows_of(C_B), 1.0)
+
+        b_gate = {}
+
+        def b_tanh(j):
+            b_gate[j] = temp.tile([P, GROUP_COLS], F32, name="b", tag="b")
+            activate_sums("b", j, b_gate[j], ACT.Tanh, rows_of(B_B), 1.0)
+
+        def input_term(j):
+            nc.vector.tensor_tensor(out=state[j][:], in0=state[j][:], in1=b_gate[j][:], op=ALU.mult)
+
+        def new_state(j):
+            nc.gpsimd.tensor_tensor(out=state[j][:], in0=state[j][:], in1=decay[j][:], op=ALU.add)
+
+        def c_times_state(j):
+            nc.vector.tensor_tensor(out=state[j][:], in0=state[j][:], in1=c_gate[j][:], op=ALU.mult)
+
+        def y_minus_deter(j):
+            nc.vector.tensor_tensor(out=mix[j][:], in0=mix[j][:], in1=state[j][:], op=ALU.add)
+
+        z_gate = {}
+
+        def z_tanh(j):
+            z_gate[j] = temp.tile([P, GROUP_COLS], F32, name="z", tag="z")
+            activate_sums("z", j, z_gate[j], ACT.Tanh, z_b_half, 0.5)
+
+        def gate_the_change(j):
+            nc.vector.scalar_tensor_tensor(
+                out=z_gate[j][:],
+                in0=z_gate[j][:],
+                scalar=1.0,
+                in1=mix[j][:],
+                op0=ALU.add,
+                op1=ALU.mult,
+            )
+
+        def add_deter(j):
+            nc.vector.scalar_tensor_tensor(
+                out=halves(mix[j]),
+                in0=halves(z_gate[j]),
+                scalar=0.5,
+                in1=group_view(deter_by_k, j),
+                op0=ALU.mult,
+                op1=ALU.add,
+            )
+
+        squares = {}
+
+        def square(j):
+            squares[j] = temp.tile([P, GROUP_COLS], F32, name="squares", tag="squares")
+            nc.scalar.activation(out=squares[j][:], in_=mix[j][:], func=ACT.Square)
+
+        def add_squares(j):
+            nc.gpsimd.tensor_tensor(
+                out=square_sum[:], in0=square_sum[:], in1=squares[j][:], op=ALU.add
+            )
+
+        def norm_gain(j):
+            for e in range(PAIR):
+                cols = slice(TOKENS * e, TOKENS * (e + 1))
+                nc.vector.tensor_scalar_mul(
+                    out=mix[j][:, cols], in0=mix[j][:, cols], scalar1=scalar_of(rows_of(NORM_W), j, e)
+                )
+
+        def when_due(step, gate, lag, stage):
+            j = step - lag - GROUPS * GATES.index(gate)
+            if 0 <= j < GROUPS:
+                stage(j)
+
+        n_groups = len(GATES) * GROUPS
+        first_log_step = GROUPS + 4
+        logs_per_step = 2
+        deepest_lag = 6
+        for step in range(n_groups + deepest_lag + 1):
+            streaming = step < n_groups
+            if step + LOADS_AHEAD < n_groups:
+                load_group(step + LOADS_AHEAD)
+            if 1 <= step <= n_groups:
+                quantise_group(step - 1)
+            if streaming:
+                transpose_group(step)
+                empty_group_bank(step, 0)
+            if 1 <= step <= n_groups:
+                multiply_group(step - 1)
+            if streaming:
+                for b in range(1, BANKS_PER_GROUP):
+                    empty_group_bank(step, b)
+            if step == 1:
+                deter_by_k = transpose_tokens(deter_rows, "deter")
+
+            when_due(step, "dt", 2, dt_argument)
+            when_due(step, "dt", 4, dt_exp)
+            log_step = step - first_log_step
+            if 0 <= log_step < GROUPS // logs_per_step:
+                if log_step == 0:
+                    nc.scalar.activation(out=a_work[:], in_=a_work[:], func=ACT.Ln, bias=one_col[:])
+                for j in range(logs_per_step * log_step, logs_per_step * (log_step + 1)):
+                    dt_log(j)
+            when_due(step, "c", 2, c_argument)
+            when_due(step, "b", 0, decay_exp)
+            when_due(step, "b", 2, b_tanh)
+            when_due(step, "z", 2, z_tanh)
+            if step == n_groups + 1:
+                nc.scalar.activation(out=sqrt_warm[:], in_=one_col[:], func=ACT.Sqrt)
+            when_due(step, "z", 5, square)
+
+            when_due(step, "z", 6, norm_gain)
+            when_due(step, "z", 6, add_squares)
+            when_due(step, "z", 4, add_deter)
+            when_due(step, "z", 3, gate_the_change)
+            when_due(step, "b", 6, y_minus_deter)
+            when_due(step, "b", 5, c_times_state)
+            when_due(step, "b", 4, new_state)
+            when_due(step, "b", 3, input_term)
+            when_due(step, "b", 1, decay_times_deter)
+            when_due(step, "c", 6, dt_times_x)
+            if 1 <= log_step <= GROUPS // logs_per_step:
+                if log_step == 1:
+                    nc.vector.tensor_tensor(
+                        out=a_work[:], in0=a_work[:], in1=rows_of(A_BASE), op=ALU.max
+                    )
+                    nc.vector.tensor_scalar_mul(out=a_neg[:], in0=a_work[:], scalar1=-1.0)
+                    nc.vector.tensor_scalar_mul(out=a_neg_dt_min[:], in0=a_work[:], scalar1=-DT_MIN)
+                for j in range(logs_per_step * (log_step - 1), logs_per_step * log_step):
+                    dt_softplus(j)
+            when_due(step, "dt", 3, skip_minus_deter)
+            when_due(step, "dt", 3, dt_cap)
+
+        token_tiles = TOKENS // P
+        totals = flip_psum.tile([P, BANK], F32, tag="flip")
+        for t in range(token_tiles):
+            for e in range(PAIR):
+                first = TOKENS * e + P * t
+                nc.tensor.matmul(
+                    out=totals[:, 32 * t : 32 * (t + 1)],
+                    lhsT=square_sum[:, first : first + P],
+                    rhs=ones[:],
+                    start=(e == 0),
+                    stop=(e == PAIR - 1),
+                )
+        rms = const.tile([P, token_tiles], F32)
+        nc.scalar.activation(
+            out=rms[:],
+            in_=totals[:, 0 : 32 * token_tiles].rearrange("p (t c) -> p t c", c=32)[:, :, 0],
+            func=ACT.Sqrt,
+            bias=eps_col[:],
+            scale=1.0 / CHANNELS,
+        )
+        inv_rms = const.tile([P, token_tiles], F32)
+        nc.vector.reciprocal(out=inv_rms[:], in_=rms[:])
+
+        groups_per_bank = BANK // GROUP_ROWS
+        for first_group in range(0, GROUPS, groups_per_bank):
+            for t in range(token_tiles):
+                bank = flip_psum.tile([P, BANK], F32, tag="flip")
+                for jj in range(groups_per_bank):
+                    for e in range(PAIR):
+                        nc.tensor.transpose(
+                            bank[:, P * (PAIR * jj + e) : P * (PAIR * jj + e + 1)],
+                            mix[first_group + jj][:, TOKENS * e + P * t : TOKENS * e + P * (t + 1)],
+                            ident[:],
+                        )
+                normed = store_pool.tile([P, BANK], F32, tag="normed")
+                normed_view = normed[:].rearrange("p (j c e) -> p j c e", j=groups_per_bank, e=PAIR)
+                bank_view = bank[:].rearrange("p (j e c) -> p j c e", j=groups_per_bank, e=PAIR)
+                if t == 0:
+                    nc.scalar.activation(
+                        out=normed_view, in_=bank_view, func=ACT.Copy, scale=inv_rms[:, t : t + 1]
+                    )
+                else:
+                    nc.vector.tensor_scalar_mul(
+                        out=normed_view, in0=bank_view, scalar1=inv_rms[:, t : t + 1]
+                    )
+                nc.sync.dma_start(
+                    out=out[P * t : P * (t + 1), GROUP_ROWS * first_group : GROUP_ROWS * first_group + BANK],
+                    in_=normed[:],
+                )

@@ -287,7 +287,7 @@ def tile_mamba2backbone_pb_kernel(
                 )
 
         def decay_times_deter(j):
-            nc.gpsimd.tensor_tensor(
+            nc.vector.tensor_tensor(
                 out=halves(decay[j]),
                 in0=halves(decay[j]),
                 in1=group_view(deter_by_k, j),
@@ -307,7 +307,7 @@ def tile_mamba2backbone_pb_kernel(
             nc.vector.tensor_tensor(out=state[j][:], in0=state[j][:], in1=b_gate[j][:], op=ALU.mult)
 
         def new_state(j):
-            nc.gpsimd.tensor_tensor(out=state[j][:], in0=state[j][:], in1=decay[j][:], op=ALU.add)
+            nc.vector.tensor_tensor(out=state[j][:], in0=state[j][:], in1=decay[j][:], op=ALU.add)
 
         def c_times_state(j):
             nc.vector.tensor_tensor(out=state[j][:], in0=state[j][:], in1=c_gate[j][:], op=ALU.mult)
@@ -348,7 +348,7 @@ def tile_mamba2backbone_pb_kernel(
             nc.scalar.activation(out=squares[j][:], in_=mix[j][:], func=ACT.Square)
 
         def add_squares(j):
-            nc.gpsimd.tensor_tensor(
+            nc.vector.tensor_tensor(
                 out=square_sum[:], in0=square_sum[:], in1=squares[j][:], op=ALU.add
             )
 

@@ -25,6 +25,10 @@ BANK = 512
 BANKS_PER_GROUP = PAIR * ROW_WORDS // BANK
 
 GATES = ["dt", "c", "b", "z"]
+VECTOR_HELPS = ["dt", "c"]
+ONES_COLS = 32
+FLIP_BANKS = 5
+SUM_BANKS = 2
 LOADS_AHEAD = 3
 EPS = 1e-4
 DT_MIN = 1e-4
@@ -56,8 +60,9 @@ def tile_mamba2backbone_pb_kernel(
         mx_pool = stack.enter_context(tc.tile_pool(name="mx", bufs=2))
         temp = stack.enter_context(tc.tile_pool(name="temp", bufs=3))
         store_pool = stack.enter_context(tc.tile_pool(name="store", bufs=4))
-        flip_psum = stack.enter_context(tc.psum_pool(name="flip", bufs=5))
-        sum_psum = stack.enter_context(tc.psum_pool(name="sums", bufs=2))
+        flip_psum = stack.enter_context(tc.psum_pool(name="flip", bufs=FLIP_BANKS))
+        sum_psum = stack.enter_context(tc.psum_pool(name="sums", bufs=SUM_BANKS))
+        late_psum = stack.enter_context(tc.psum_pool(name="late", bufs=1))
         stack.enter_context(tc.manual_schedule())
 
         ident = const.tile([P, P], F32)
@@ -67,10 +72,8 @@ def tile_mamba2backbone_pb_kernel(
         eps_col = const.tile([P, 1], F32)
         nc.vector.memset(eps_col[:], EPS)
         sqrt_warm = const.tile([P, 1], F32)
-        ones = const.tile([P, 32], F32)
+        ones = const.tile([P, ONES_COLS], F32)
         nc.vector.memset(ones[:], 1.0)
-        square_sum = keep.tile([P, GROUP_COLS], F32)
-        nc.vector.memset(square_sum[:], 0.0)
 
         def load_rows(rows_view):
             rows = raw_pool.tile([P, PAIR * CHANNELS], BF16, tag="raw")
@@ -84,6 +87,7 @@ def tile_mamba2backbone_pb_kernel(
             rows = weights[gate][GROUP_ROWS * j : GROUP_ROWS * (j + 1), :]
             raw[index] = load_rows(rows.rearrange("(p e) k -> p e k", e=PAIR))
 
+        load_group(0)
         x_rows = load_rows(x.rearrange("(t p) k -> p t k", p=P))
         vector_rows = const.tile([P, GROUP_ROWS], BF16)
         nc.vector.memset(vector_rows[:], 0.0)
@@ -92,13 +96,12 @@ def tile_mamba2backbone_pb_kernel(
                 out=vector_rows[GROUPS * i : GROUPS * (i + 1), :],
                 in_=vector.rearrange("(j c) -> j c", j=GROUPS),
             )
-        load_group(0)
         load_group(1)
-        deter_rows = load_rows(deter.rearrange("(t p) k -> p t k", p=P))
         load_group(2)
+        deter_rows = load_rows(deter.rearrange("(t p) k -> p t k", p=P))
 
-        def empty_bank(position, out_words, bank_view):
-            if position % BANKS_PER_GROUP == 0:
+        def empty_bank(on_vector, out_words, bank_view):
+            if on_vector:
                 nc.vector.tensor_copy(out=out_words, in_=bank_view)
             else:
                 nc.scalar.copy(out=out_words, in_=bank_view)
@@ -118,7 +121,7 @@ def tile_mamba2backbone_pb_kernel(
                         )
                 by_k = keep.tile([P, TOKENS * PACK], BF16, name="%s%d" % (name, g), align_bytes=64)
                 empty_bank(
-                    g,
+                    g == 0,
                     by_k[:].bitcast(F32).rearrange("p (t u) -> p t u", u=PAIR),
                     bank[:].rearrange("p (u t) -> p t u", u=PAIR),
                 )
@@ -129,33 +132,35 @@ def tile_mamba2backbone_pb_kernel(
             g, u = j // PAIR, j % PAIR
             return tiles[g][:].rearrange("p (t c) -> p c t", c=PACK)[:, PAIR * u : PAIR * (u + 1), :]
 
-        x_by_k = transpose_tokens(x_rows, "x")
         x_codes = keep.tile([P, PASSES * TOKENS], U32, align_bytes=64)
         x_scales = keep.tile([P, PASSES * TOKENS], U8, align_bytes=64)
-        for g in range(PASSES):
-            cols = slice(TOKENS * g, TOKENS * (g + 1))
-            nc.vector.quantize_mx(
-                out=x_codes[:, cols].bitcast(FP8X4), scales=x_scales[:, cols], in_=x_by_k[g][:]
-            )
 
-        vector_bank = flip_psum.tile([P, BANK], F32, tag="flip")
-        nc.tensor.transpose(vector_bank[:, 0:P], vector_rows[:].bitcast(F32), ident[:])
+        def quantise_x():
+            for g in range(PASSES):
+                cols = slice(TOKENS * g, TOKENS * (g + 1))
+                nc.vector.quantize_mx(
+                    out=x_codes[:, cols].bitcast(FP8X4), scales=x_scales[:, cols], in_=x_by_k[g][:]
+                )
+
         table = const.tile([P, PAIR * P], F32)
-        nc.vector.tensor_copy(out=table[:], in_=vector_bank[:, 0:P].bitcast(BF16))
+        z_b_half = const.tile([P, PAIR * GROUPS], F32)
+        a_work = const.tile([P, PAIR * GROUPS], F32)
+        a_neg = const.tile([P, PAIR * GROUPS], F32)
+        a_neg_dt_min = const.tile([P, PAIR * GROUPS], F32)
+
+        def transpose_vectors():
+            vector_bank = flip_psum.tile([P, BANK], F32, tag="flip")
+            nc.tensor.transpose(vector_bank[:, 0:P], vector_rows[:].bitcast(F32), ident[:])
+            nc.vector.tensor_copy(out=table[:], in_=vector_bank[:, 0:P].bitcast(BF16))
+            nc.vector.tensor_scalar_mul(out=z_b_half[:], in0=rows_of(Z_B), scalar1=0.5)
+            nc.vector.tensor_scalar_min(out=a_work[:], in0=rows_of(A_BASE), scalar1=EXP_CAP)
+            nc.scalar.activation(out=a_work[:], in_=a_work[:], func=ACT.Exp)
 
         def rows_of(which):
             return table[:, PAIR * GROUPS * which : PAIR * GROUPS * (which + 1)]
 
         def scalar_of(columns, j, e):
             return columns[:, PAIR * j + e : PAIR * j + e + 1]
-
-        z_b_half = const.tile([P, PAIR * GROUPS], F32)
-        nc.vector.tensor_scalar_mul(out=z_b_half[:], in0=rows_of(Z_B), scalar1=0.5)
-        a_work = const.tile([P, PAIR * GROUPS], F32)
-        nc.vector.tensor_scalar_min(out=a_work[:], in0=rows_of(A_BASE), scalar1=EXP_CAP)
-        nc.scalar.activation(out=a_work[:], in_=a_work[:], func=ACT.Exp)
-        a_neg = const.tile([P, PAIR * GROUPS], F32)
-        a_neg_dt_min = const.tile([P, PAIR * GROUPS], F32)
 
         def group_tiles(name):
             return [keep.tile([P, GROUP_COLS], F32, name="%s%d" % (name, j)) for j in range(GROUPS)]
@@ -166,7 +171,6 @@ def tile_mamba2backbone_pb_kernel(
         soft = group_tiles("soft")
         decay = group_tiles("decay")
         state = group_tiles("state")
-        c_gate = group_tiles("cgate")
         mix = group_tiles("mix")
 
         banks = {}
@@ -194,7 +198,7 @@ def tile_mamba2backbone_pb_kernel(
 
         def empty_group_bank(index, b):
             empty_bank(
-                b,
+                b == 0 and GATES[index // GROUPS] in VECTOR_HELPS,
                 grouped[index][:]
                 .bitcast(F32)[:, BANK * b : BANK * (b + 1)]
                 .rearrange("p (g n u) -> p g n u", g=PAIR, u=PAIR),
@@ -202,18 +206,22 @@ def tile_mamba2backbone_pb_kernel(
             )
 
         def quantise_group(index):
-            codes[index] = mx_pool.tile(
-                [P, PAIR * PASSES * P], U32, name="codes", tag="codes", align_bytes=64
+            if GATES[index // GROUPS] == "c":
+                pool, suffix = keep, "_c%d" % (index % GROUPS)
+            else:
+                pool, suffix = mx_pool, ""
+            codes[index] = pool.tile(
+                [P, PAIR * PASSES * P], U32, name="codes" + suffix, align_bytes=64
             )
-            scales[index] = mx_pool.tile(
-                [P, PAIR * PASSES * P], U8, name="scales", tag="scales", align_bytes=64
+            scales[index] = pool.tile(
+                [P, PAIR * PASSES * P], U8, name="scales" + suffix, align_bytes=64
             )
             nc.vector.quantize_mx(
                 out=codes[index][:].bitcast(FP8X4), scales=scales[index][:], in_=grouped[index][:]
             )
 
-        def multiply_group(index):
-            sums[index] = sum_psum.tile([P, GROUP_COLS], F32, name="sums", tag="sums")
+        def multiply_group(index, pool, tag):
+            sums[index] = pool.tile([P, GROUP_COLS], F32, name=tag, tag=tag)
             for e in range(PAIR):
                 for g in range(PASSES):
                     w_cols = slice(P * (PASSES * e + g), P * (PASSES * e + g + 1))
@@ -294,8 +302,8 @@ def tile_mamba2backbone_pb_kernel(
                 op=ALU.mult,
             )
 
-        def c_argument(j):
-            activate_sums("c", j, c_gate[j], ACT.Identity, rows_of(C_B), 1.0)
+        def c_matmuls(j):
+            multiply_group(GROUPS * GATES.index("c") + j, late_psum, "late")
 
         b_gate = {}
 
@@ -310,7 +318,16 @@ def tile_mamba2backbone_pb_kernel(
             nc.vector.tensor_tensor(out=state[j][:], in0=state[j][:], in1=decay[j][:], op=ALU.add)
 
         def c_times_state(j):
-            nc.vector.tensor_tensor(out=state[j][:], in0=state[j][:], in1=c_gate[j][:], op=ALU.mult)
+            for e in range(PAIR):
+                cols = slice(TOKENS * e, TOKENS * (e + 1))
+                nc.vector.scalar_tensor_tensor(
+                    out=state[j][:, cols],
+                    in0=sums[GROUPS * GATES.index("c") + j][:, cols],
+                    scalar=scalar_of(rows_of(C_B), j, e),
+                    in1=state[j][:, cols],
+                    op0=ALU.add,
+                    op1=ALU.mult,
+                )
 
         def y_minus_deter(j):
             nc.vector.tensor_tensor(out=mix[j][:], in0=mix[j][:], in1=state[j][:], op=ALU.add)
@@ -347,10 +364,23 @@ def tile_mamba2backbone_pb_kernel(
             squares[j] = temp.tile([P, GROUP_COLS], F32, name="squares", tag="squares")
             nc.scalar.activation(out=squares[j][:], in_=mix[j][:], func=ACT.Square)
 
+        token_tiles = TOKENS // P
+        totals = {}
+
         def add_squares(j):
-            nc.vector.tensor_tensor(
-                out=square_sum[:], in0=square_sum[:], in1=squares[j][:], op=ALU.add
-            )
+            if j == 0:
+                totals[0] = late_psum.tile([P, BANK], F32, name="totals", tag="late")
+            for t in range(token_tiles):
+                first_col = ONES_COLS * (token_tiles * j + t)
+                for e in range(PAIR):
+                    first = TOKENS * e + P * t
+                    nc.tensor.matmul(
+                        out=totals[0][:, first_col : first_col + ONES_COLS],
+                        lhsT=squares[j][:, first : first + P],
+                        rhs=ones[:],
+                        start=(e == 0),
+                        stop=(e == PAIR - 1),
+                    )
 
         def norm_gain(j):
             for e in range(PAIR):
@@ -358,6 +388,46 @@ def tile_mamba2backbone_pb_kernel(
                 nc.vector.tensor_scalar_mul(
                     out=mix[j][:, cols], in0=mix[j][:, cols], scalar1=scalar_of(rows_of(NORM_W), j, e)
                 )
+
+        rms = const.tile([P, token_tiles], F32)
+        inv_rms = const.tile([P, token_tiles], F32)
+
+        def finish_norm():
+            square_sum = const.tile([P, token_tiles], F32)
+            nc.vector.tensor_reduce(
+                out=square_sum[:],
+                in_=totals[0][:].rearrange("p (j t c) -> p t j c", t=token_tiles, c=ONES_COLS)[
+                    :, :, :, 0
+                ],
+                axis=mybir.AxisListType.X,
+                op=ALU.add,
+            )
+            nc.scalar.activation(
+                out=rms[:], in_=square_sum[:], func=ACT.Sqrt, bias=eps_col[:], scale=1.0 / CHANNELS
+            )
+            nc.vector.reciprocal(out=inv_rms[:], in_=rms[:])
+
+        free_banks = (
+            FLIP_BANKS * [(flip_psum, "flip")] + SUM_BANKS * [(sum_psum, "sums")] + [(late_psum, "late")]
+        )
+        groups_per_bank = BANK // GROUP_ROWS
+        out_banks = []
+
+        def flip_back(j):
+            if j % groups_per_bank == groups_per_bank - 1:
+                first_group = j - (groups_per_bank - 1)
+                for t in range(token_tiles):
+                    pool, tag = free_banks[len(out_banks)]
+                    bank = pool.tile([P, BANK], F32, name="out_bank", tag=tag)
+                    for jj in range(groups_per_bank):
+                        for e in range(PAIR):
+                            first = TOKENS * e + P * t
+                            nc.tensor.transpose(
+                                bank[:, P * (PAIR * jj + e) : P * (PAIR * jj + e + 1)],
+                                mix[first_group + jj][:, first : first + P],
+                                ident[:],
+                            )
+                    out_banks.append((bank, first_group, t))
 
         def when_due(step, gate, lag, stage):
             j = step - lag - GROUPS * GATES.index(gate)
@@ -367,23 +437,26 @@ def tile_mamba2backbone_pb_kernel(
         n_groups = len(GATES) * GROUPS
         first_log_step = GROUPS + 4
         logs_per_step = 2
-        deepest_lag = 6
-        for step in range(n_groups + deepest_lag + 1):
-            streaming = step < n_groups
-            if step + LOADS_AHEAD < n_groups:
-                load_group(step + LOADS_AHEAD)
+        last_group = n_groups - 1
+        deepest_lag = 7
+        for step in range(n_groups + deepest_lag):
             if 1 <= step <= n_groups:
                 quantise_group(step - 1)
-            if streaming:
+            if step < n_groups:
                 transpose_group(step)
-                empty_group_bank(step, 0)
-            if 1 <= step <= n_groups:
-                multiply_group(step - 1)
-            if streaming:
-                for b in range(1, BANKS_PER_GROUP):
+            if 1 <= step <= n_groups and GATES[(step - 1) // GROUPS] != "c":
+                multiply_group(step - 1, sum_psum, "sums")
+            if step < n_groups:
+                for b in range(BANKS_PER_GROUP):
                     empty_group_bank(step, b)
-            if step == 1:
+            if step == 0:
+                x_by_k = transpose_tokens(x_rows, "x")
+                quantise_x()
+                transpose_vectors()
+            if step == 2:
                 deter_by_k = transpose_tokens(deter_rows, "deter")
+            if step + LOADS_AHEAD < n_groups:
+                load_group(step + LOADS_AHEAD)
 
             when_due(step, "dt", 2, dt_argument)
             when_due(step, "dt", 4, dt_exp)
@@ -393,16 +466,14 @@ def tile_mamba2backbone_pb_kernel(
                     nc.scalar.activation(out=a_work[:], in_=a_work[:], func=ACT.Ln, bias=one_col[:])
                 for j in range(logs_per_step * log_step, logs_per_step * (log_step + 1)):
                     dt_log(j)
-            when_due(step, "c", 2, c_argument)
             when_due(step, "b", 0, decay_exp)
             when_due(step, "b", 2, b_tanh)
             when_due(step, "z", 2, z_tanh)
-            if step == n_groups + 1:
+            if step == last_group + 2:
                 nc.scalar.activation(out=sqrt_warm[:], in_=one_col[:], func=ACT.Sqrt)
             when_due(step, "z", 5, square)
 
             when_due(step, "z", 6, norm_gain)
-            when_due(step, "z", 6, add_squares)
             when_due(step, "z", 4, add_deter)
             when_due(step, "z", 3, gate_the_change)
             when_due(step, "b", 6, y_minus_deter)
@@ -423,52 +494,25 @@ def tile_mamba2backbone_pb_kernel(
             when_due(step, "dt", 3, skip_minus_deter)
             when_due(step, "dt", 3, dt_cap)
 
-        token_tiles = TOKENS // P
-        totals = flip_psum.tile([P, BANK], F32, tag="flip")
-        for t in range(token_tiles):
-            for e in range(PAIR):
-                first = TOKENS * e + P * t
-                nc.tensor.matmul(
-                    out=totals[:, 32 * t : 32 * (t + 1)],
-                    lhsT=square_sum[:, first : first + P],
-                    rhs=ones[:],
-                    start=(e == 0),
-                    stop=(e == PAIR - 1),
-                )
-        rms = const.tile([P, token_tiles], F32)
-        nc.scalar.activation(
-            out=rms[:],
-            in_=totals[:, 0 : 32 * token_tiles].rearrange("p (t c) -> p t c", c=32)[:, :, 0],
-            func=ACT.Sqrt,
-            bias=eps_col[:],
-            scale=1.0 / CHANNELS,
-        )
-        inv_rms = const.tile([P, token_tiles], F32)
-        nc.vector.reciprocal(out=inv_rms[:], in_=rms[:])
+            when_due(step, "b", 4, c_matmuls)
+            when_due(step, "z", 6, add_squares)
+            when_due(step, "z", 7, flip_back)
+            if step == last_group + 6:
+                finish_norm()
 
-        groups_per_bank = BANK // GROUP_ROWS
-        for first_group in range(0, GROUPS, groups_per_bank):
-            for t in range(token_tiles):
-                bank = flip_psum.tile([P, BANK], F32, tag="flip")
-                for jj in range(groups_per_bank):
-                    for e in range(PAIR):
-                        nc.tensor.transpose(
-                            bank[:, P * (PAIR * jj + e) : P * (PAIR * jj + e + 1)],
-                            mix[first_group + jj][:, TOKENS * e + P * t : TOKENS * e + P * (t + 1)],
-                            ident[:],
-                        )
-                normed = store_pool.tile([P, BANK], F32, tag="normed")
-                normed_view = normed[:].rearrange("p (j c e) -> p j c e", j=groups_per_bank, e=PAIR)
-                bank_view = bank[:].rearrange("p (j e c) -> p j c e", j=groups_per_bank, e=PAIR)
-                if t == 0:
-                    nc.scalar.activation(
-                        out=normed_view, in_=bank_view, func=ACT.Copy, scale=inv_rms[:, t : t + 1]
-                    )
-                else:
-                    nc.vector.tensor_scalar_mul(
-                        out=normed_view, in0=bank_view, scalar1=inv_rms[:, t : t + 1]
-                    )
-                nc.sync.dma_start(
-                    out=out[P * t : P * (t + 1), GROUP_ROWS * first_group : GROUP_ROWS * first_group + BANK],
-                    in_=normed[:],
+        for bank, first_group, t in out_banks:
+            normed = store_pool.tile([P, BANK], F32, tag="normed")
+            normed_view = normed[:].rearrange("p (j c e) -> p j c e", j=groups_per_bank, e=PAIR)
+            bank_view = bank[:].rearrange("p (j e c) -> p j c e", j=groups_per_bank, e=PAIR)
+            if t == 0:
+                nc.scalar.activation(
+                    out=normed_view, in_=bank_view, func=ACT.Copy, scale=inv_rms[:, t : t + 1]
                 )
+            else:
+                nc.vector.tensor_scalar_mul(
+                    out=normed_view, in0=bank_view, scalar1=inv_rms[:, t : t + 1]
+                )
+            first_channel = GROUP_ROWS * first_group
+            nc.sync.dma_start(
+                out=out[P * t : P * (t + 1), first_channel : first_channel + BANK], in_=normed[:]
+            )

@@ -22,7 +22,8 @@ GROUPS = CHANNELS // GROUP_ROWS
 GROUP_COLS = PAIR * TOKENS
 ROW_WORDS = CHANNELS // PAIR
 BANK = 512
-BANKS_PER_GROUP = PAIR * ROW_WORDS // BANK
+BANKS_PER_ROW = ROW_WORDS // BANK
+BANKS_PER_GROUP = PAIR * BANKS_PER_ROW
 
 GATES = ["dt", "c", "b", "z"]
 VECTOR_HELPS = ["dt", "c"]
@@ -179,10 +180,9 @@ def tile_mamba2backbone_pb_kernel(
         scales = {}
         sums = {}
 
-        def transpose_group(index):
+        def transpose_row(index, e):
             words = raw[index][:].bitcast(F32)
-            banks[index] = []
-            for b in range(BANKS_PER_GROUP):
+            for b in range(BANKS_PER_ROW * e, BANKS_PER_ROW * (e + 1)):
                 bank = flip_psum.tile([P, BANK], F32, tag="flip")
                 for piece in range(BANK // P):
                     first_word = BANK * b + P * piece
@@ -191,10 +191,7 @@ def tile_mamba2backbone_pb_kernel(
                         words[:, first_word : first_word + P],
                         ident[:],
                     )
-                banks[index].append(bank)
-            grouped[index] = grouped_pool.tile(
-                [P, PAIR * CHANNELS], BF16, name="grouped", tag="grouped", align_bytes=64
-            )
+                banks[index, b] = bank
 
         def empty_group_bank(index, b):
             empty_bank(
@@ -202,7 +199,7 @@ def tile_mamba2backbone_pb_kernel(
                 grouped[index][:]
                 .bitcast(F32)[:, BANK * b : BANK * (b + 1)]
                 .rearrange("p (g n u) -> p g n u", g=PAIR, u=PAIR),
-                banks[index][b][:].rearrange("p (g u n) -> p g n u", g=PAIR, u=PAIR),
+                banks[index, b][:].rearrange("p (g u n) -> p g n u", g=PAIR, u=PAIR),
             )
 
         def quantise_group(index):
@@ -220,21 +217,19 @@ def tile_mamba2backbone_pb_kernel(
                 out=codes[index][:].bitcast(FP8X4), scales=scales[index][:], in_=grouped[index][:]
             )
 
-        def multiply_group(index, pool, tag):
-            sums[index] = pool.tile([P, GROUP_COLS], F32, name=tag, tag=tag)
-            for e in range(PAIR):
-                for g in range(PASSES):
-                    w_cols = slice(P * (PASSES * e + g), P * (PASSES * e + g + 1))
-                    x_cols = slice(TOKENS * g, TOKENS * (g + 1))
-                    nc.tensor.matmul_mx(
-                        out=sums[index][:, TOKENS * e : TOKENS * (e + 1)],
-                        lhsT=codes[index][:, w_cols].bitcast(FP8X4),
-                        lhsT_scale=scales[index][:, w_cols],
-                        rhs=x_codes[:, x_cols].bitcast(FP8X4),
-                        rhs_scale=x_scales[:, x_cols],
-                        start=(g == 0),
-                        stop=(g == PASSES - 1),
-                    )
+        def multiply_row(index, e):
+            for g in range(PASSES):
+                w_cols = slice(P * (PASSES * e + g), P * (PASSES * e + g + 1))
+                x_cols = slice(TOKENS * g, TOKENS * (g + 1))
+                nc.tensor.matmul_mx(
+                    out=sums[index][:, TOKENS * e : TOKENS * (e + 1)],
+                    lhsT=codes[index][:, w_cols].bitcast(FP8X4),
+                    lhsT_scale=scales[index][:, w_cols],
+                    rhs=x_codes[:, x_cols].bitcast(FP8X4),
+                    rhs_scale=x_scales[:, x_cols],
+                    start=(g == 0),
+                    stop=(g == PASSES - 1),
+                )
 
         def activate_sums(gate, j, out_tile, func, bias_columns, scale):
             for e in range(PAIR):
@@ -303,7 +298,10 @@ def tile_mamba2backbone_pb_kernel(
             )
 
         def c_matmuls(j):
-            multiply_group(GROUPS * GATES.index("c") + j, late_psum, "late")
+            index = GROUPS * GATES.index("c") + j
+            sums[index] = late_psum.tile([P, GROUP_COLS], F32, name="c_sums", tag="late")
+            for e in range(PAIR):
+                multiply_row(index, e)
 
         b_gate = {}
 
@@ -442,11 +440,18 @@ def tile_mamba2backbone_pb_kernel(
         for step in range(n_groups + deepest_lag):
             if 1 <= step <= n_groups:
                 quantise_group(step - 1)
+            multiplying = 1 <= step <= n_groups and GATES[(step - 1) // GROUPS] != "c"
+            if multiplying:
+                sums[step - 1] = sum_psum.tile([P, GROUP_COLS], F32, name="sums", tag="sums")
+            for e in range(PAIR):
+                if step < n_groups:
+                    transpose_row(step, e)
+                if multiplying:
+                    multiply_row(step - 1, e)
             if step < n_groups:
-                transpose_group(step)
-            if 1 <= step <= n_groups and GATES[(step - 1) // GROUPS] != "c":
-                multiply_group(step - 1, sum_psum, "sums")
-            if step < n_groups:
+                grouped[step] = grouped_pool.tile(
+                    [P, PAIR * CHANNELS], BF16, name="grouped", tag="grouped", align_bytes=64
+                )
                 for b in range(BANKS_PER_GROUP):
                     empty_group_bank(step, b)
             if step == 0:

@@ -26,10 +26,12 @@ BANKS_PER_ROW = ROW_WORDS // BANK
 BANKS_PER_GROUP = PAIR * BANKS_PER_ROW
 
 GATES = ["dt", "c", "b", "z"]
-VECTOR_HELPS = ["dt", "c"]
+VECTOR_HELP_GROUPS = 20
+MULTIPLY_LAG = 2
 ONES_COLS = 32
 FLIP_BANKS = 5
 SUM_BANKS = 2
+LATE_BANKS = 1
 LOADS_AHEAD = 3
 EPS = 1e-4
 DT_MIN = 1e-4
@@ -63,7 +65,7 @@ def tile_mamba2backbone_pb_kernel(
         store_pool = stack.enter_context(tc.tile_pool(name="store", bufs=4))
         flip_psum = stack.enter_context(tc.psum_pool(name="flip", bufs=FLIP_BANKS))
         sum_psum = stack.enter_context(tc.psum_pool(name="sums", bufs=SUM_BANKS))
-        late_psum = stack.enter_context(tc.psum_pool(name="late", bufs=1))
+        late_psum = stack.enter_context(tc.psum_pool(name="late", bufs=LATE_BANKS))
         stack.enter_context(tc.manual_schedule())
 
         ident = const.tile([P, P], F32)
@@ -122,7 +124,7 @@ def tile_mamba2backbone_pb_kernel(
                         )
                 by_k = keep.tile([P, TOKENS * PACK], BF16, name="%s%d" % (name, g), align_bytes=64)
                 empty_bank(
-                    g == 0,
+                    g % 2 == 0,
                     by_k[:].bitcast(F32).rearrange("p (t u) -> p t u", u=PAIR),
                     bank[:].rearrange("p (u t) -> p t u", u=PAIR),
                 )
@@ -155,7 +157,6 @@ def tile_mamba2backbone_pb_kernel(
             nc.vector.tensor_copy(out=table[:], in_=vector_bank[:, 0:P].bitcast(BF16))
             nc.vector.tensor_scalar_mul(out=z_b_half[:], in0=rows_of(Z_B), scalar1=0.5)
             nc.vector.tensor_scalar_min(out=a_work[:], in0=rows_of(A_BASE), scalar1=EXP_CAP)
-            nc.scalar.activation(out=a_work[:], in_=a_work[:], func=ACT.Exp)
 
         def rows_of(which):
             return table[:, PAIR * GROUPS * which : PAIR * GROUPS * (which + 1)]
@@ -195,7 +196,7 @@ def tile_mamba2backbone_pb_kernel(
 
         def empty_group_bank(index, b):
             empty_bank(
-                b == 0 and GATES[index // GROUPS] in VECTOR_HELPS,
+                b == 0 and index < VECTOR_HELP_GROUPS,
                 grouped[index][:]
                 .bitcast(F32)[:, BANK * b : BANK * (b + 1)]
                 .rearrange("p (g n u) -> p g n u", g=PAIR, u=PAIR),
@@ -406,26 +407,26 @@ def tile_mamba2backbone_pb_kernel(
             nc.vector.reciprocal(out=inv_rms[:], in_=rms[:])
 
         free_banks = (
-            FLIP_BANKS * [(flip_psum, "flip")] + SUM_BANKS * [(sum_psum, "sums")] + [(late_psum, "late")]
+            FLIP_BANKS * [(flip_psum, "flip")]
+            + SUM_BANKS * [(sum_psum, "sums")]
+            + LATE_BANKS * [(late_psum, "late")]
         )
         groups_per_bank = BANK // GROUP_ROWS
         out_banks = []
 
-        def flip_back(j):
-            if j % groups_per_bank == groups_per_bank - 1:
-                first_group = j - (groups_per_bank - 1)
-                for t in range(token_tiles):
-                    pool, tag = free_banks[len(out_banks)]
-                    bank = pool.tile([P, BANK], F32, name="out_bank", tag=tag)
-                    for jj in range(groups_per_bank):
-                        for e in range(PAIR):
-                            first = TOKENS * e + P * t
-                            nc.tensor.transpose(
-                                bank[:, P * (PAIR * jj + e) : P * (PAIR * jj + e + 1)],
-                                mix[first_group + jj][:, first : first + P],
-                                ident[:],
-                            )
-                    out_banks.append((bank, first_group, t))
+        def flip_back(first_group):
+            for t in range(token_tiles):
+                pool, tag = free_banks[len(out_banks)]
+                bank = pool.tile([P, BANK], F32, name="out_bank", tag=tag)
+                for jj in range(groups_per_bank):
+                    for e in range(PAIR):
+                        first = TOKENS * e + P * t
+                        nc.tensor.transpose(
+                            bank[:, P * (PAIR * jj + e) : P * (PAIR * jj + e + 1)],
+                            mix[first_group + jj][:, first : first + P],
+                            ident[:],
+                        )
+                out_banks.append((bank, first_group, t))
 
         def when_due(step, gate, lag, stage):
             j = step - lag - GROUPS * GATES.index(gate)
@@ -433,21 +434,22 @@ def tile_mamba2backbone_pb_kernel(
                 stage(j)
 
         n_groups = len(GATES) * GROUPS
-        first_log_step = GROUPS + 4
+        first_log_step = GROUPS + 5
         logs_per_step = 2
         last_group = n_groups - 1
-        deepest_lag = 7
+        deepest_lag = 11
         for step in range(n_groups + deepest_lag):
             if 1 <= step <= n_groups:
                 quantise_group(step - 1)
-            multiplying = 1 <= step <= n_groups and GATES[(step - 1) // GROUPS] != "c"
-            if multiplying:
-                sums[step - 1] = sum_psum.tile([P, GROUP_COLS], F32, name="sums", tag="sums")
-            for e in range(PAIR):
-                if step < n_groups:
+
+            if step < n_groups:
+                for e in range(PAIR):
                     transpose_row(step, e)
-                if multiplying:
-                    multiply_row(step - 1, e)
+            ready = step - MULTIPLY_LAG
+            if 0 <= ready < n_groups and GATES[ready // GROUPS] != "c":
+                sums[ready] = sum_psum.tile([P, GROUP_COLS], F32, name="sums", tag="sums")
+                for e in range(PAIR):
+                    multiply_row(ready, e)
             if step < n_groups:
                 grouped[step] = grouped_pool.tile(
                     [P, PAIR * CHANNELS], BF16, name="grouped", tag="grouped", align_bytes=64
@@ -456,37 +458,40 @@ def tile_mamba2backbone_pb_kernel(
                     empty_group_bank(step, b)
             if step == 0:
                 x_by_k = transpose_tokens(x_rows, "x")
+            if step == 1:
                 quantise_x()
-                transpose_vectors()
             if step == 2:
                 deter_by_k = transpose_tokens(deter_rows, "deter")
+                transpose_vectors()
             if step + LOADS_AHEAD < n_groups:
                 load_group(step + LOADS_AHEAD)
 
-            when_due(step, "dt", 2, dt_argument)
-            when_due(step, "dt", 4, dt_exp)
+            when_due(step, "dt", 3, dt_argument)
+            if step == 5:
+                nc.scalar.activation(out=a_work[:], in_=a_work[:], func=ACT.Exp)
+            when_due(step, "dt", 5, dt_exp)
             log_step = step - first_log_step
             if 0 <= log_step < GROUPS // logs_per_step:
                 if log_step == 0:
                     nc.scalar.activation(out=a_work[:], in_=a_work[:], func=ACT.Ln, bias=one_col[:])
                 for j in range(logs_per_step * log_step, logs_per_step * (log_step + 1)):
                     dt_log(j)
-            when_due(step, "b", 0, decay_exp)
-            when_due(step, "b", 2, b_tanh)
-            when_due(step, "z", 2, z_tanh)
-            if step == last_group + 2:
+            when_due(step, "b", 1, decay_exp)
+            when_due(step, "b", 3, b_tanh)
+            when_due(step, "z", 3, z_tanh)
+            when_due(step, "z", 6, square)
+            if step == last_group + 6:
                 nc.scalar.activation(out=sqrt_warm[:], in_=one_col[:], func=ACT.Sqrt)
-            when_due(step, "z", 5, square)
 
-            when_due(step, "z", 6, norm_gain)
-            when_due(step, "z", 4, add_deter)
-            when_due(step, "z", 3, gate_the_change)
-            when_due(step, "b", 6, y_minus_deter)
-            when_due(step, "b", 5, c_times_state)
-            when_due(step, "b", 4, new_state)
-            when_due(step, "b", 3, input_term)
-            when_due(step, "b", 1, decay_times_deter)
-            when_due(step, "c", 6, dt_times_x)
+            when_due(step, "z", 11, norm_gain)
+            when_due(step, "z", 5, add_deter)
+            when_due(step, "z", 4, gate_the_change)
+            when_due(step, "b", 8, y_minus_deter)
+            when_due(step, "b", 6, c_times_state)
+            when_due(step, "b", 5, new_state)
+            when_due(step, "b", 4, input_term)
+            when_due(step, "b", 2, decay_times_deter)
+            when_due(step, "c", 7, dt_times_x)
             if 1 <= log_step <= GROUPS // logs_per_step:
                 if log_step == 1:
                     nc.vector.tensor_tensor(
@@ -497,14 +502,14 @@ def tile_mamba2backbone_pb_kernel(
                 for j in range(logs_per_step * (log_step - 1), logs_per_step * log_step):
                     dt_softplus(j)
             when_due(step, "dt", 3, skip_minus_deter)
-            when_due(step, "dt", 3, dt_cap)
+            when_due(step, "dt", 4, dt_cap)
 
-            when_due(step, "b", 4, c_matmuls)
-            when_due(step, "z", 6, add_squares)
-            when_due(step, "z", 7, flip_back)
-            if step == last_group + 6:
-                finish_norm()
+            when_due(step, "b", 5, c_matmuls)
+            when_due(step, "z", 7, add_squares)
 
+        finish_norm()
+        for first_group in range(0, GROUPS, groups_per_bank):
+            flip_back(first_group)
         for bank, first_group, t in out_banks:
             normed = store_pool.tile([P, BANK], F32, tag="normed")
             normed_view = normed[:].rearrange("p (j c e) -> p j c e", j=groups_per_bank, e=PAIR)

@@ -13,6 +13,7 @@ ALU = mybir.AluOpType
 
 P = 128
 TOKENS = 256
+TOKEN_TILES = TOKENS // P
 CHANNELS = 2048
 PAIR = 2
 PACK = 4
@@ -22,17 +23,21 @@ GROUPS = CHANNELS // GROUP_ROWS
 GROUP_COLS = PAIR * TOKENS
 ROW_WORDS = CHANNELS // PAIR
 BANK = 512
-BANKS_PER_ROW = ROW_WORDS // BANK
-BANKS_PER_GROUP = PAIR * BANKS_PER_ROW
+BANKS_PER_GROUP = PAIR * ROW_WORDS // BANK
+GROUPS_PER_BANK = BANK // GROUP_ROWS
 
 GATES = ["dt", "c", "b", "z"]
-VECTOR_HELP_GROUPS = 20
-MULTIPLY_LAG = 2
-ONES_COLS = 32
-FLIP_BANKS = 5
+N_GROUPS = len(GATES) * GROUPS
+LOADS_AHEAD = 3
+
 SUM_BANKS = 2
 LATE_BANKS = 1
-LOADS_AHEAD = 3
+FLIP_BANKS = 8 - SUM_BANKS - LATE_BANKS
+
+MULTIPLY_LAG = 2
+SUMS_LAG = MULTIPLY_LAG + 1
+
+ONES_COLS = BANK // (GROUPS * TOKEN_TILES)
 EPS = 1e-4
 DT_MIN = 1e-4
 EXP_CAP = 20.0
@@ -54,6 +59,9 @@ def tile_mamba2backbone_pb_kernel(
     nc = tc.nc
     weights = {"dt": dt_w, "c": c_w, "b": b_w, "z": z_w}
     vectors = [a_base, dt_b, b_b, c_b, z_b, skip, norm_w]
+
+    def first_step(gate):
+        return GROUPS * GATES.index(gate)
 
     with ExitStack() as stack:
         const = stack.enter_context(tc.tile_pool(name="const", bufs=1))
@@ -78,17 +86,17 @@ def tile_mamba2backbone_pb_kernel(
         ones = const.tile([P, ONES_COLS], F32)
         nc.vector.memset(ones[:], 1.0)
 
-        def load_rows(rows_view):
+        def load_rows(dram_view):
             rows = raw_pool.tile([P, PAIR * CHANNELS], BF16, tag="raw")
-            nc.sync.dma_start(out=rows[:].rearrange("p (r k) -> p r k", r=PAIR), in_=rows_view)
+            nc.sync.dma_start(out=rows[:].rearrange("p (r k) -> p r k", r=PAIR), in_=dram_view)
             return rows
 
         raw = {}
 
         def load_group(index):
             gate, j = GATES[index // GROUPS], index % GROUPS
-            rows = weights[gate][GROUP_ROWS * j : GROUP_ROWS * (j + 1), :]
-            raw[index] = load_rows(rows.rearrange("(p e) k -> p e k", e=PAIR))
+            group_rows = weights[gate][GROUP_ROWS * j : GROUP_ROWS * (j + 1), :]
+            raw[index] = load_rows(group_rows.rearrange("(p e) k -> p e k", e=PAIR))
 
         load_group(0)
         x_rows = load_rows(x.rearrange("(t p) k -> p t k", p=P))
@@ -115,7 +123,7 @@ def tile_mamba2backbone_pb_kernel(
             for g in range(PASSES):
                 bank = flip_psum.tile([P, BANK], F32, tag="flip")
                 for u in range(PAIR):
-                    for t in range(TOKENS // P):
+                    for t in range(TOKEN_TILES):
                         first_word = ROW_WORDS * t + P * (PAIR * g + u)
                         nc.tensor.transpose(
                             bank[:, TOKENS * u + P * t : TOKENS * u + P * (t + 1)],
@@ -133,7 +141,8 @@ def tile_mamba2backbone_pb_kernel(
 
         def group_view(tiles, j):
             g, u = j // PAIR, j % PAIR
-            return tiles[g][:].rearrange("p (t c) -> p c t", c=PACK)[:, PAIR * u : PAIR * (u + 1), :]
+            by_value = tiles[g][:].rearrange("p (t c) -> p c t", c=PACK)
+            return by_value[:, PAIR * u : PAIR * (u + 1), :]
 
         x_codes = keep.tile([P, PASSES * TOKENS], U32, align_bytes=64)
         x_scales = keep.tile([P, PASSES * TOKENS], U8, align_bytes=64)
@@ -151,18 +160,18 @@ def tile_mamba2backbone_pb_kernel(
         a_neg = const.tile([P, PAIR * GROUPS], F32)
         a_neg_dt_min = const.tile([P, PAIR * GROUPS], F32)
 
+        def columns_of(which):
+            return table[:, PAIR * GROUPS * which : PAIR * GROUPS * (which + 1)]
+
+        def channel_scalar(columns, j, e):
+            return columns[:, PAIR * j + e : PAIR * j + e + 1]
+
         def transpose_vectors():
             vector_bank = flip_psum.tile([P, BANK], F32, tag="flip")
             nc.tensor.transpose(vector_bank[:, 0:P], vector_rows[:].bitcast(F32), ident[:])
             nc.vector.tensor_copy(out=table[:], in_=vector_bank[:, 0:P].bitcast(BF16))
-            nc.vector.tensor_scalar_mul(out=z_b_half[:], in0=rows_of(Z_B), scalar1=0.5)
-            nc.vector.tensor_scalar_min(out=a_work[:], in0=rows_of(A_BASE), scalar1=EXP_CAP)
-
-        def rows_of(which):
-            return table[:, PAIR * GROUPS * which : PAIR * GROUPS * (which + 1)]
-
-        def scalar_of(columns, j, e):
-            return columns[:, PAIR * j + e : PAIR * j + e + 1]
+            nc.vector.tensor_scalar_mul(out=z_b_half[:], in0=columns_of(Z_B), scalar1=0.5)
+            nc.vector.tensor_scalar_min(out=a_work[:], in0=columns_of(A_BASE), scalar1=EXP_CAP)
 
         def group_tiles(name):
             return [keep.tile([P, GROUP_COLS], F32, name="%s%d" % (name, j)) for j in range(GROUPS)]
@@ -181,9 +190,9 @@ def tile_mamba2backbone_pb_kernel(
         scales = {}
         sums = {}
 
-        def transpose_row(index, e):
+        def transpose_group(index):
             words = raw[index][:].bitcast(F32)
-            for b in range(BANKS_PER_ROW * e, BANKS_PER_ROW * (e + 1)):
+            for b in range(BANKS_PER_GROUP):
                 bank = flip_psum.tile([P, BANK], F32, tag="flip")
                 for piece in range(BANK // P):
                     first_word = BANK * b + P * piece
@@ -194,14 +203,20 @@ def tile_mamba2backbone_pb_kernel(
                     )
                 banks[index, b] = bank
 
-        def empty_group_bank(index, b):
-            empty_bank(
-                b == 0 and index < VECTOR_HELP_GROUPS,
-                grouped[index][:]
-                .bitcast(F32)[:, BANK * b : BANK * (b + 1)]
-                .rearrange("p (g n u) -> p g n u", g=PAIR, u=PAIR),
-                banks[index, b][:].rearrange("p (g u n) -> p g n u", g=PAIR, u=PAIR),
+        vector_helps_until = first_step("b") + SUMS_LAG + 1
+
+        def empty_group(index):
+            grouped[index] = grouped_pool.tile(
+                [P, PAIR * CHANNELS], BF16, name="grouped", tag="grouped", align_bytes=64
             )
+            for b in range(BANKS_PER_GROUP):
+                empty_bank(
+                    b == 0 and index < vector_helps_until,
+                    grouped[index][:]
+                    .bitcast(F32)[:, BANK * b : BANK * (b + 1)]
+                    .rearrange("p (g n u) -> p g n u", g=PAIR, u=PAIR),
+                    banks[index, b][:].rearrange("p (g u n) -> p g n u", g=PAIR, u=PAIR),
+                )
 
         def quantise_group(index):
             if GATES[index // GROUPS] == "c":
@@ -218,33 +233,35 @@ def tile_mamba2backbone_pb_kernel(
                 out=codes[index][:].bitcast(FP8X4), scales=scales[index][:], in_=grouped[index][:]
             )
 
-        def multiply_row(index, e):
-            for g in range(PASSES):
-                w_cols = slice(P * (PASSES * e + g), P * (PASSES * e + g + 1))
-                x_cols = slice(TOKENS * g, TOKENS * (g + 1))
-                nc.tensor.matmul_mx(
-                    out=sums[index][:, TOKENS * e : TOKENS * (e + 1)],
-                    lhsT=codes[index][:, w_cols].bitcast(FP8X4),
-                    lhsT_scale=scales[index][:, w_cols],
-                    rhs=x_codes[:, x_cols].bitcast(FP8X4),
-                    rhs_scale=x_scales[:, x_cols],
-                    start=(g == 0),
-                    stop=(g == PASSES - 1),
-                )
+        def multiply_group(index, pool, tag):
+            sums[index] = pool.tile([P, GROUP_COLS], F32, name=tag, tag=tag)
+            for e in range(PAIR):
+                for g in range(PASSES):
+                    w_cols = slice(P * (PASSES * e + g), P * (PASSES * e + g + 1))
+                    x_cols = slice(TOKENS * g, TOKENS * (g + 1))
+                    nc.tensor.matmul_mx(
+                        out=sums[index][:, TOKENS * e : TOKENS * (e + 1)],
+                        lhsT=codes[index][:, w_cols].bitcast(FP8X4),
+                        lhsT_scale=scales[index][:, w_cols],
+                        rhs=x_codes[:, x_cols].bitcast(FP8X4),
+                        rhs_scale=x_scales[:, x_cols],
+                        start=(g == 0),
+                        stop=(g == PASSES - 1),
+                    )
 
         def activate_sums(gate, j, out_tile, func, bias_columns, scale):
             for e in range(PAIR):
                 cols = slice(TOKENS * e, TOKENS * (e + 1))
                 nc.scalar.activation(
                     out=out_tile[:, cols],
-                    in_=sums[GROUPS * GATES.index(gate) + j][:, cols],
+                    in_=sums[first_step(gate) + j][:, cols],
                     func=func,
-                    bias=scalar_of(bias_columns, j, e),
+                    bias=channel_scalar(bias_columns, j, e),
                     scale=scale,
                 )
 
         def dt_argument(j):
-            activate_sums("dt", j, soft[j], ACT.Identity, rows_of(DT_B), 1.0)
+            activate_sums("dt", j, soft[j], ACT.Identity, columns_of(DT_B), 1.0)
 
         def dt_cap(j):
             nc.vector.tensor_scalar_min(out=decay[j][:], in0=soft[j][:], scalar1=EXP_CAP)
@@ -263,7 +280,7 @@ def tile_mamba2backbone_pb_kernel(
                 nc.vector.scalar_tensor_tensor(
                     out=halves(mix[j])[:, e, :],
                     in0=group_view(x_by_k, j)[:, e, :],
-                    scalar=scalar_of(rows_of(SKIP), j, e),
+                    scalar=channel_scalar(columns_of(SKIP), j, e),
                     in1=group_view(deter_by_k, j)[:, e, :],
                     op0=ALU.mult,
                     op1=ALU.subtract,
@@ -286,8 +303,8 @@ def tile_mamba2backbone_pb_kernel(
                     out=decay[j][:, cols],
                     in_=soft[j][:, cols],
                     func=ACT.Exp,
-                    bias=scalar_of(a_neg_dt_min, j, e),
-                    scale=scalar_of(a_neg, j, e),
+                    bias=channel_scalar(a_neg_dt_min, j, e),
+                    scale=channel_scalar(a_neg, j, e),
                 )
 
         def decay_times_deter(j):
@@ -298,17 +315,11 @@ def tile_mamba2backbone_pb_kernel(
                 op=ALU.mult,
             )
 
-        def c_matmuls(j):
-            index = GROUPS * GATES.index("c") + j
-            sums[index] = late_psum.tile([P, GROUP_COLS], F32, name="c_sums", tag="late")
-            for e in range(PAIR):
-                multiply_row(index, e)
-
         b_gate = {}
 
         def b_tanh(j):
             b_gate[j] = temp.tile([P, GROUP_COLS], F32, name="b", tag="b")
-            activate_sums("b", j, b_gate[j], ACT.Tanh, rows_of(B_B), 1.0)
+            activate_sums("b", j, b_gate[j], ACT.Tanh, columns_of(B_B), 1.0)
 
         def input_term(j):
             nc.vector.tensor_tensor(out=state[j][:], in0=state[j][:], in1=b_gate[j][:], op=ALU.mult)
@@ -316,13 +327,16 @@ def tile_mamba2backbone_pb_kernel(
         def new_state(j):
             nc.vector.tensor_tensor(out=state[j][:], in0=state[j][:], in1=decay[j][:], op=ALU.add)
 
+        def c_matmuls(j):
+            multiply_group(first_step("c") + j, late_psum, "late")
+
         def c_times_state(j):
             for e in range(PAIR):
                 cols = slice(TOKENS * e, TOKENS * (e + 1))
                 nc.vector.scalar_tensor_tensor(
                     out=state[j][:, cols],
-                    in0=sums[GROUPS * GATES.index("c") + j][:, cols],
-                    scalar=scalar_of(rows_of(C_B), j, e),
+                    in0=sums[first_step("c") + j][:, cols],
+                    scalar=channel_scalar(columns_of(C_B), j, e),
                     in1=state[j][:, cols],
                     op0=ALU.add,
                     op1=ALU.mult,
@@ -363,14 +377,13 @@ def tile_mamba2backbone_pb_kernel(
             squares[j] = temp.tile([P, GROUP_COLS], F32, name="squares", tag="squares")
             nc.scalar.activation(out=squares[j][:], in_=mix[j][:], func=ACT.Square)
 
-        token_tiles = TOKENS // P
         totals = {}
 
         def add_squares(j):
             if j == 0:
                 totals[0] = late_psum.tile([P, BANK], F32, name="totals", tag="late")
-            for t in range(token_tiles):
-                first_col = ONES_COLS * (token_tiles * j + t)
+            for t in range(TOKEN_TILES):
+                first_col = ONES_COLS * (TOKEN_TILES * j + t)
                 for e in range(PAIR):
                     first = TOKENS * e + P * t
                     nc.tensor.matmul(
@@ -381,44 +394,113 @@ def tile_mamba2backbone_pb_kernel(
                         stop=(e == PAIR - 1),
                     )
 
-        def norm_gain(j):
+        def one_a_step(step, first, stage):
+            if 0 <= step - first < GROUPS:
+                stage(step - first)
+
+        def when_due(step, gate, lag, stage):
+            one_a_step(step, first_step(gate) + lag, stage)
+
+        first_exp_step = first_step("dt") + SUMS_LAG + 2
+        first_log_step = first_exp_step + GROUPS
+        logs_per_step = 2
+        log_steps = GROUPS // logs_per_step
+        last_stage_lag = SUMS_LAG + 4
+        for step in range(N_GROUPS + last_stage_lag):
+            if 1 <= step <= N_GROUPS:
+                quantise_group(step - 1)
+
+            if step < N_GROUPS:
+                transpose_group(step)
+            ready = step - MULTIPLY_LAG
+            if 0 <= ready < N_GROUPS and GATES[ready // GROUPS] != "c":
+                multiply_group(ready, sum_psum, "sums")
+            if step < N_GROUPS:
+                empty_group(step)
+
+            if step == 0:
+                x_by_k = transpose_tokens(x_rows, "x")
+            if step == MULTIPLY_LAG - 1:
+                quantise_x()
+            if step == SUMS_LAG - 1:
+                deter_by_k = transpose_tokens(deter_rows, "deter")
+                transpose_vectors()
+            if step + LOADS_AHEAD < N_GROUPS:
+                load_group(step + LOADS_AHEAD)
+
+            when_due(step, "dt", SUMS_LAG, dt_argument)
+            if step == first_exp_step:
+                nc.scalar.activation(out=a_work[:], in_=a_work[:], func=ACT.Exp)
+            one_a_step(step, first_exp_step, dt_exp)
+            log_step = step - first_log_step
+            if log_step == 0:
+                nc.scalar.activation(out=a_work[:], in_=a_work[:], func=ACT.Ln, bias=one_col[:])
+            if 0 <= log_step < log_steps:
+                for j in range(logs_per_step * log_step, logs_per_step * (log_step + 1)):
+                    dt_log(j)
+            one_a_step(step, first_log_step + log_steps, decay_exp)
+            when_due(step, "b", SUMS_LAG, b_tanh)
+            when_due(step, "z", SUMS_LAG, z_tanh)
+            when_due(step, "z", SUMS_LAG + 3, square)
+
+            when_due(step, "z", SUMS_LAG + 2, add_deter)
+            when_due(step, "z", SUMS_LAG + 1, gate_the_change)
+            when_due(step, "b", SUMS_LAG + 4, y_minus_deter)
+            when_due(step, "b", SUMS_LAG + 3, c_times_state)
+            when_due(step, "b", SUMS_LAG + 2, new_state)
+            when_due(step, "b", SUMS_LAG + 1, input_term)
+            one_a_step(step, first_log_step + log_steps + 1, decay_times_deter)
+            one_a_step(step, first_log_step + 2, dt_times_x)
+            if log_step == 1:
+                nc.vector.tensor_tensor(
+                    out=a_work[:], in0=a_work[:], in1=columns_of(A_BASE), op=ALU.max
+                )
+                nc.vector.tensor_scalar_mul(out=a_neg[:], in0=a_work[:], scalar1=-1.0)
+                nc.vector.tensor_scalar_mul(out=a_neg_dt_min[:], in0=a_work[:], scalar1=-DT_MIN)
+            if 1 <= log_step <= log_steps:
+                for j in range(logs_per_step * (log_step - 1), logs_per_step * log_step):
+                    dt_softplus(j)
+            one_a_step(step, SUMS_LAG, skip_minus_deter)
+            when_due(step, "dt", SUMS_LAG + 1, dt_cap)
+
+            when_due(step, "b", SUMS_LAG + 2, c_matmuls)
+            when_due(step, "z", last_stage_lag, add_squares)
+
+        nc.scalar.activation(out=sqrt_warm[:], in_=one_col[:], func=ACT.Sqrt)
+        for j in range(GROUPS):
             for e in range(PAIR):
                 cols = slice(TOKENS * e, TOKENS * (e + 1))
                 nc.vector.tensor_scalar_mul(
-                    out=mix[j][:, cols], in0=mix[j][:, cols], scalar1=scalar_of(rows_of(NORM_W), j, e)
+                    out=mix[j][:, cols],
+                    in0=mix[j][:, cols],
+                    scalar1=channel_scalar(columns_of(NORM_W), j, e),
                 )
-
-        rms = const.tile([P, token_tiles], F32)
-        inv_rms = const.tile([P, token_tiles], F32)
-
-        def finish_norm():
-            square_sum = const.tile([P, token_tiles], F32)
-            nc.vector.tensor_reduce(
-                out=square_sum[:],
-                in_=totals[0][:].rearrange("p (j t c) -> p t j c", t=token_tiles, c=ONES_COLS)[
-                    :, :, :, 0
-                ],
-                axis=mybir.AxisListType.X,
-                op=ALU.add,
-            )
-            nc.scalar.activation(
-                out=rms[:], in_=square_sum[:], func=ACT.Sqrt, bias=eps_col[:], scale=1.0 / CHANNELS
-            )
-            nc.vector.reciprocal(out=inv_rms[:], in_=rms[:])
+        square_sum = const.tile([P, TOKEN_TILES], F32)
+        by_token_tile = totals[0][:].rearrange("p (j t c) -> p t j c", t=TOKEN_TILES, c=ONES_COLS)
+        nc.vector.tensor_reduce(
+            out=square_sum[:],
+            in_=by_token_tile[:, :, :, 0],
+            axis=mybir.AxisListType.X,
+            op=ALU.add,
+        )
+        rms = const.tile([P, TOKEN_TILES], F32)
+        nc.scalar.activation(
+            out=rms[:], in_=square_sum[:], func=ACT.Sqrt, bias=eps_col[:], scale=1.0 / CHANNELS
+        )
+        inv_rms = const.tile([P, TOKEN_TILES], F32)
+        nc.vector.reciprocal(out=inv_rms[:], in_=rms[:])
 
         free_banks = (
             FLIP_BANKS * [(flip_psum, "flip")]
             + SUM_BANKS * [(sum_psum, "sums")]
             + LATE_BANKS * [(late_psum, "late")]
         )
-        groups_per_bank = BANK // GROUP_ROWS
         out_banks = []
-
-        def flip_back(first_group):
-            for t in range(token_tiles):
+        for first_group in range(0, GROUPS, GROUPS_PER_BANK):
+            for t in range(TOKEN_TILES):
                 pool, tag = free_banks[len(out_banks)]
                 bank = pool.tile([P, BANK], F32, name="out_bank", tag=tag)
-                for jj in range(groups_per_bank):
+                for jj in range(GROUPS_PER_BANK):
                     for e in range(PAIR):
                         first = TOKENS * e + P * t
                         nc.tensor.transpose(
@@ -427,93 +509,10 @@ def tile_mamba2backbone_pb_kernel(
                             ident[:],
                         )
                 out_banks.append((bank, first_group, t))
-
-        def when_due(step, gate, lag, stage):
-            j = step - lag - GROUPS * GATES.index(gate)
-            if 0 <= j < GROUPS:
-                stage(j)
-
-        n_groups = len(GATES) * GROUPS
-        first_log_step = GROUPS + 5
-        logs_per_step = 2
-        last_group = n_groups - 1
-        deepest_lag = 11
-        for step in range(n_groups + deepest_lag):
-            if 1 <= step <= n_groups:
-                quantise_group(step - 1)
-
-            if step < n_groups:
-                for e in range(PAIR):
-                    transpose_row(step, e)
-            ready = step - MULTIPLY_LAG
-            if 0 <= ready < n_groups and GATES[ready // GROUPS] != "c":
-                sums[ready] = sum_psum.tile([P, GROUP_COLS], F32, name="sums", tag="sums")
-                for e in range(PAIR):
-                    multiply_row(ready, e)
-            if step < n_groups:
-                grouped[step] = grouped_pool.tile(
-                    [P, PAIR * CHANNELS], BF16, name="grouped", tag="grouped", align_bytes=64
-                )
-                for b in range(BANKS_PER_GROUP):
-                    empty_group_bank(step, b)
-            if step == 0:
-                x_by_k = transpose_tokens(x_rows, "x")
-            if step == 1:
-                quantise_x()
-            if step == 2:
-                deter_by_k = transpose_tokens(deter_rows, "deter")
-                transpose_vectors()
-            if step + LOADS_AHEAD < n_groups:
-                load_group(step + LOADS_AHEAD)
-
-            when_due(step, "dt", 3, dt_argument)
-            if step == 5:
-                nc.scalar.activation(out=a_work[:], in_=a_work[:], func=ACT.Exp)
-            when_due(step, "dt", 5, dt_exp)
-            log_step = step - first_log_step
-            if 0 <= log_step < GROUPS // logs_per_step:
-                if log_step == 0:
-                    nc.scalar.activation(out=a_work[:], in_=a_work[:], func=ACT.Ln, bias=one_col[:])
-                for j in range(logs_per_step * log_step, logs_per_step * (log_step + 1)):
-                    dt_log(j)
-            when_due(step, "b", 1, decay_exp)
-            when_due(step, "b", 3, b_tanh)
-            when_due(step, "z", 3, z_tanh)
-            when_due(step, "z", 6, square)
-            if step == last_group + 6:
-                nc.scalar.activation(out=sqrt_warm[:], in_=one_col[:], func=ACT.Sqrt)
-
-            when_due(step, "z", 11, norm_gain)
-            when_due(step, "z", 5, add_deter)
-            when_due(step, "z", 4, gate_the_change)
-            when_due(step, "b", 8, y_minus_deter)
-            when_due(step, "b", 6, c_times_state)
-            when_due(step, "b", 5, new_state)
-            when_due(step, "b", 4, input_term)
-            when_due(step, "b", 2, decay_times_deter)
-            when_due(step, "c", 7, dt_times_x)
-            if 1 <= log_step <= GROUPS // logs_per_step:
-                if log_step == 1:
-                    nc.vector.tensor_tensor(
-                        out=a_work[:], in0=a_work[:], in1=rows_of(A_BASE), op=ALU.max
-                    )
-                    nc.vector.tensor_scalar_mul(out=a_neg[:], in0=a_work[:], scalar1=-1.0)
-                    nc.vector.tensor_scalar_mul(out=a_neg_dt_min[:], in0=a_work[:], scalar1=-DT_MIN)
-                for j in range(logs_per_step * (log_step - 1), logs_per_step * log_step):
-                    dt_softplus(j)
-            when_due(step, "dt", 3, skip_minus_deter)
-            when_due(step, "dt", 4, dt_cap)
-
-            when_due(step, "b", 5, c_matmuls)
-            when_due(step, "z", 7, add_squares)
-
-        finish_norm()
-        for first_group in range(0, GROUPS, groups_per_bank):
-            flip_back(first_group)
         for bank, first_group, t in out_banks:
             normed = store_pool.tile([P, BANK], F32, tag="normed")
-            normed_view = normed[:].rearrange("p (j c e) -> p j c e", j=groups_per_bank, e=PAIR)
-            bank_view = bank[:].rearrange("p (j e c) -> p j c e", j=groups_per_bank, e=PAIR)
+            normed_view = normed[:].rearrange("p (j c e) -> p j c e", j=GROUPS_PER_BANK, e=PAIR)
+            bank_view = bank[:].rearrange("p (j e c) -> p j c e", j=GROUPS_PER_BANK, e=PAIR)
             if t == 0:
                 nc.scalar.activation(
                     out=normed_view, in_=bank_view, func=ACT.Copy, scale=inv_rms[:, t : t + 1]

from contextlib import ExitStack

import concourse.mybir as mybir
from concourse.masks import make_identity

F32 = mybir.dt.float32
BF16 = mybir.dt.bfloat16
U32 = mybir.dt.uint32
U8 = mybir.dt.uint8
FP8X4 = mybir.dt.float8_e4m3fn_x4
ACT = mybir.ActivationFunctionType
ALU = mybir.AluOpType

P = 128
TOKENS = 256
TOKEN_TILES = TOKENS // P
CHANNELS = 2048
PAIR = 2
PACK = 4
PASSES = CHANNELS // (P * PACK)
GROUP_ROWS = PAIR * P
GROUPS = CHANNELS // GROUP_ROWS
GROUP_COLS = PAIR * TOKENS
ROW_WORDS = CHANNELS // PAIR
BANK = 512
BANKS_PER_GROUP = PAIR * ROW_WORDS // BANK
GROUPS_PER_BANK = BANK // GROUP_ROWS

GATES = ["dt", "c", "b", "z"]
N_GROUPS = len(GATES) * GROUPS
LOADS_AHEAD = 3

SUM_BANKS = 2
LATE_BANKS = 1
FLIP_BANKS = 8 - SUM_BANKS - LATE_BANKS

MULTIPLY_LAG = 2
SUMS_LAG = MULTIPLY_LAG + 1

ONES_COLS = BANK // (GROUPS * TOKEN_TILES)
EPS = 1e-4
DT_MIN = 1e-4
EXP_CAP = 20.0

A_BASE = 0
DT_B = 1
B_B = 2
C_B = 3
Z_B = 4
SKIP = 5
NORM_W = 6

FLOPS = 4 * 2 * TOKENS * CHANNELS * CHANNELS


def tile_mamba2backbone_pb_kernel(
    tc, x, deter, a_base, dt_w, dt_b, b_w, b_b, c_w, c_b, z_w, z_b, skip, norm_w, out
):
    nc = tc.nc
    weights = {"dt": dt_w, "c": c_w, "b": b_w, "z": z_w}
    vectors = [a_base, dt_b, b_b, c_b, z_b, skip, norm_w]

    def first_step(gate):
        return GROUPS * GATES.index(gate)

    with ExitStack() as stack:
        const = stack.enter_context(tc.tile_pool(name="const", bufs=1))
        keep = stack.enter_context(tc.tile_pool(name="keep", bufs=1))
        raw_pool = stack.enter_context(tc.tile_pool(name="raw", bufs=LOADS_AHEAD + 2))
        grouped_pool = stack.enter_context(tc.tile_pool(name="grouped", bufs=3))
        mx_pool = stack.enter_context(tc.tile_pool(name="mx", bufs=2))
        temp = stack.enter_context(tc.tile_pool(name="temp", bufs=3))
        store_pool = stack.enter_context(tc.tile_pool(name="store", bufs=4))
        flip_psum = stack.enter_context(tc.psum_pool(name="flip", bufs=FLIP_BANKS))
        sum_psum = stack.enter_context(tc.psum_pool(name="sums", bufs=SUM_BANKS))
        late_psum = stack.enter_context(tc.psum_pool(name="late", bufs=LATE_BANKS))
        stack.enter_context(tc.manual_schedule())

        ident = const.tile([P, P], F32)
        make_identity(nc, ident[:])
        one_col = const.tile([P, 1], F32)
        nc.vector.memset(one_col[:], 1.0)
        eps_col = const.tile([P, 1], F32)
        nc.vector.memset(eps_col[:], EPS)
        sqrt_warm = const.tile([P, 1], F32)
        ones = const.tile([P, ONES_COLS], F32)
        nc.vector.memset(ones[:], 1.0)

        def load_rows(dram_view):
            rows = raw_pool.tile([P, PAIR * CHANNELS], BF16, tag="raw")
            nc.sync.dma_start(out=rows[:].rearrange("p (r k) -> p r k", r=PAIR), in_=dram_view)
            return rows

        raw = {}

        def load_group(index):
            gate, j = GATES[index // GROUPS], index % GROUPS
            group_rows = weights[gate][GROUP_ROWS * j : GROUP_ROWS * (j + 1), :]
            raw[index] = load_rows(group_rows.rearrange("(p e) k -> p e k", e=PAIR))

        load_group(0)
        x_rows = load_rows(x.rearrange("(t p) k -> p t k", p=P))
        vector_rows = const.tile([P, GROUP_ROWS], BF16)
        nc.vector.memset(vector_rows[:], 0.0)
        for i, vector in enumerate(vectors):
            nc.scalar.dma_start(
                out=vector_rows[GROUPS * i : GROUPS * (i + 1), :],
                in_=vector.rearrange("(j c) -> j c", j=GROUPS),
            )
        load_group(1)
        load_group(2)
        deter_rows = load_rows(deter.rearrange("(t p) k -> p t k", p=P))

        def empty_bank(on_vector, out_words, bank_view):
            if on_vector:
                nc.vector.tensor_copy(out=out_words, in_=bank_view)
            else:
                nc.scalar.copy(out=out_words, in_=bank_view)

        def transpose_tokens(rows, name):
            words = rows[:].bitcast(F32)
            tiles = []
            for g in range(PASSES):
                bank = flip_psum.tile([P, BANK], F32, tag="flip")
                for u in range(PAIR):
                    for t in range(TOKEN_TILES):
                        first_word = ROW_WORDS * t + P * (PAIR * g + u)
                        nc.tensor.transpose(
                            bank[:, TOKENS * u + P * t : TOKENS * u + P * (t + 1)],
                            words[:, first_word : first_word + P],
                            ident[:],
                        )
                by_k = keep.tile([P, TOKENS * PACK], BF16, name="%s%d" % (name, g), align_bytes=64)
                empty_bank(
                    g % 2 == 0,
                    by_k[:].bitcast(F32).rearrange("p (t u) -> p t u", u=PAIR),
                    bank[:].rearrange("p (u t) -> p t u", u=PAIR),
                )
                tiles.append(by_k)
            return tiles

        def group_view(tiles, j):
            g, u = j // PAIR, j % PAIR
            by_value = tiles[g][:].rearrange("p (t c) -> p c t", c=PACK)
            return by_value[:, PAIR * u : PAIR * (u + 1), :]

        x_codes = keep.tile([P, PASSES * TOKENS], U32, align_bytes=64)
        x_scales = keep.tile([P, PASSES * TOKENS], U8, align_bytes=64)

        def quantise_x():
            for g in range(PASSES):
                cols = slice(TOKENS * g, TOKENS * (g + 1))
                nc.vector.quantize_mx(
                    out=x_codes[:, cols].bitcast(FP8X4), scales=x_scales[:, cols], in_=x_by_k[g][:]
                )

        table = const.tile([P, PAIR * P], F32)
        z_b_half = const.tile([P, PAIR * GROUPS], F32)
        a_work = const.tile([P, PAIR * GROUPS], F32)
        a_neg = const.tile([P, PAIR * GROUPS], F32)
        a_neg_dt_min = const.tile([P, PAIR * GROUPS], F32)

        def columns_of(which):
            return table[:, PAIR * GROUPS * which : PAIR * GROUPS * (which + 1)]

        def channel_scalar(columns, j, e):
            return columns[:, PAIR * j + e : PAIR * j + e + 1]

        def transpose_vectors():
            vector_bank = flip_psum.tile([P, BANK], F32, tag="flip")
            nc.tensor.transpose(vector_bank[:, 0:P], vector_rows[:].bitcast(F32), ident[:])
            nc.vector.tensor_copy(out=table[:], in_=vector_bank[:, 0:P].bitcast(BF16))
            nc.vector.tensor_scalar_mul(out=z_b_half[:], in0=columns_of(Z_B), scalar1=0.5)
            nc.vector.tensor_scalar_min(out=a_work[:], in0=columns_of(A_BASE), scalar1=EXP_CAP)

        def group_tiles(name):
            return [keep.tile([P, GROUP_COLS], F32, name="%s%d" % (name, j)) for j in range(GROUPS)]

        def halves(group_tile):
            return group_tile[:].rearrange("p (e t) -> p e t", e=PAIR)

        soft = group_tiles("soft")
        decay = group_tiles("decay")
        state = group_tiles("state")
        mix = group_tiles("mix")

        banks = {}
        grouped = {}
        codes = {}
        scales = {}
        sums = {}

        def transpose_group(index):
            words = raw[index][:].bitcast(F32)
            for b in range(BANKS_PER_GROUP):
                bank = flip_psum.tile([P, BANK], F32, tag="flip")
                for piece in range(BANK // P):
                    first_word = BANK * b + P * piece
                    nc.tensor.transpose(
                        bank[:, P * piece : P * (piece + 1)],
                        words[:, first_word : first_word + P],
                        ident[:],
                    )
                banks[index, b] = bank

        vector_helps_until = first_step("b") + SUMS_LAG + 1

        def empty_group(index):
            grouped[index] = grouped_pool.tile(
                [P, PAIR * CHANNELS], BF16, name="grouped", tag="grouped", align_bytes=64
            )
            for b in range(BANKS_PER_GROUP):
                empty_bank(
                    b == 0 and index < vector_helps_until,
                    grouped[index][:]
                    .bitcast(F32)[:, BANK * b : BANK * (b + 1)]
                    .rearrange("p (g n u) -> p g n u", g=PAIR, u=PAIR),
                    banks[index, b][:].rearrange("p (g u n) -> p g n u", g=PAIR, u=PAIR),
                )

        def quantise_group(index):
            if GATES[index // GROUPS] == "c":
                pool, suffix = keep, "_c%d" % (index % GROUPS)
            else:
                pool, suffix = mx_pool, ""
            codes[index] = pool.tile(
                [P, PAIR * PASSES * P], U32, name="codes" + suffix, align_bytes=64
            )
            scales[index] = pool.tile(
                [P, PAIR * PASSES * P], U8, name="scales" + suffix, align_bytes=64
            )
            nc.vector.quantize_mx(
                out=codes[index][:].bitcast(FP8X4), scales=scales[index][:], in_=grouped[index][:]
            )

        def multiply_group(index, pool, tag):
            sums[index] = pool.tile([P, GROUP_COLS], F32, name=tag, tag=tag)
            for e in range(PAIR):
                for g in range(PASSES):
                    w_cols = slice(P * (PASSES * e + g), P * (PASSES * e + g + 1))
                    x_cols = slice(TOKENS * g, TOKENS * (g + 1))
                    nc.tensor.matmul_mx(
                        out=sums[index][:, TOKENS * e : TOKENS * (e + 1)],
                        lhsT=codes[index][:, w_cols].bitcast(FP8X4),
                        lhsT_scale=scales[index][:, w_cols],
                        rhs=x_codes[:, x_cols].bitcast(FP8X4),
                        rhs_scale=x_scales[:, x_cols],
                        start=(g == 0),
                        stop=(g == PASSES - 1),
                    )

        def activate_sums(gate, j, out_tile, func, bias_columns, scale):
            for e in range(PAIR):
                cols = slice(TOKENS * e, TOKENS * (e + 1))
                nc.scalar.activation(
                    out=out_tile[:, cols],
                    in_=sums[first_step(gate) + j][:, cols],
                    func=func,
                    bias=channel_scalar(bias_columns, j, e),
                    scale=scale,
                )

        def dt_argument(j):
            activate_sums("dt", j, soft[j], ACT.Identity, columns_of(DT_B), 1.0)

        def dt_cap(j):
            nc.vector.tensor_scalar_min(out=decay[j][:], in0=soft[j][:], scalar1=EXP_CAP)

        def dt_exp(j):
            nc.scalar.activation(out=decay[j][:], in_=decay[j][:], func=ACT.Exp)

        def dt_log(j):
            nc.scalar.activation(out=decay[j][:], in_=decay[j][:], func=ACT.Ln, bias=one_col[:])

        def dt_softplus(j):
            nc.vector.tensor_tensor(out=soft[j][:], in0=soft[j][:], in1=decay[j][:], op=ALU.max)

        def skip_minus_deter(j):
            for e in range(PAIR):
                nc.vector.scalar_tensor_tensor(
                    out=halves(mix[j])[:, e, :],
                    in0=group_view(x_by_k, j)[:, e, :],
                    scalar=channel_scalar(columns_of(SKIP), j, e),
                    in1=group_view(deter_by_k, j)[:, e, :],
                    op0=ALU.mult,
                    op1=ALU.subtract,
                )

        def dt_times_x(j):
            nc.vector.scalar_tensor_tensor(
                out=halves(state[j]),
                in0=halves(soft[j]),
                scalar=DT_MIN,
                in1=group_view(x_by_k, j),
                op0=ALU.add,
                op1=ALU.mult,
            )

        def decay_exp(j):
            for e in range(PAIR):
                cols = slice(TOKENS * e, TOKENS * (e + 1))
                nc.scalar.activation(
                    out=decay[j][:, cols],
                    in_=soft[j][:, cols],
                    func=ACT.Exp,
                    bias=channel_scalar(a_neg_dt_min, j, e),
                    scale=channel_scalar(a_neg, j, e),
                )

        def decay_times_deter(j):
            nc.vector.tensor_tensor(
                out=halves(decay[j]),
                in0=halves(decay[j]),
                in1=group_view(deter_by_k, j),
                op=ALU.mult,
            )

        b_gate = {}

        def b_tanh(j):
            b_gate[j] = temp.tile([P, GROUP_COLS], F32, name="b", tag="b")
            activate_sums("b", j, b_gate[j], ACT.Tanh, columns_of(B_B), 1.0)

        def input_term(j):
            nc.vector.tensor_tensor(out=state[j][:], in0=state[j][:], in1=b_gate[j][:], op=ALU.mult)

        def new_state(j):
            nc.vector.tensor_tensor(out=state[j][:], in0=state[j][:], in1=decay[j][:], op=ALU.add)

        def c_matmuls(j):
            multiply_group(first_step("c") + j, late_psum, "late")

        def c_times_state(j):
            for e in range(PAIR):
                cols = slice(TOKENS * e, TOKENS * (e + 1))
                nc.vector.scalar_tensor_tensor(
                    out=state[j][:, cols],
                    in0=sums[first_step("c") + j][:, cols],
                    scalar=channel_scalar(columns_of(C_B), j, e),
                    in1=state[j][:, cols],
                    op0=ALU.add,
                    op1=ALU.mult,
                )

        def y_minus_deter(j):
            nc.vector.tensor_tensor(out=mix[j][:], in0=mix[j][:], in1=state[j][:], op=ALU.add)

        z_gate = {}

        def z_tanh(j):
            z_gate[j] = temp.tile([P, GROUP_COLS], F32, name="z", tag="z")
            activate_sums("z", j, z_gate[j], ACT.Tanh, z_b_half, 0.5)

        def gate_the_change(j):
            nc.vector.scalar_tensor_tensor(
                out=z_gate[j][:],
                in0=z_gate[j][:],
                scalar=1.0,
                in1=mix[j][:],
                op0=ALU.add,
                op1=ALU.mult,
            )

        def add_deter(j):
            nc.vector.scalar_tensor_tensor(
                out=halves(mix[j]),
                in0=halves(z_gate[j]),
                scalar=0.5,
                in1=group_view(deter_by_k, j),
                op0=ALU.mult,
                op1=ALU.add,
            )

        squares = {}

        def square(j):
            squares[j] = temp.tile([P, GROUP_COLS], F32, name="squares", tag="squares")
            nc.scalar.activation(out=squares[j][:], in_=mix[j][:], func=ACT.Square)

        totals = {}

        def add_squares(j):
            if j == 0:
                totals[0] = late_psum.tile([P, BANK], F32, name="totals", tag="late")
            for t in range(TOKEN_TILES):
                first_col = ONES_COLS * (TOKEN_TILES * j + t)
                for e in range(PAIR):
                    first = TOKENS * e + P * t
                    nc.tensor.matmul(
                        out=totals[0][:, first_col : first_col + ONES_COLS],
                        lhsT=squares[j][:, first : first + P],
                        rhs=ones[:],
                        start=(e == 0),
                        stop=(e == PAIR - 1),
                    )

        def one_a_step(step, first, stage):
            if 0 <= step - first < GROUPS:
                stage(step - first)

        def when_due(step, gate, lag, stage):
            one_a_step(step, first_step(gate) + lag, stage)

        first_exp_step = first_step("dt") + SUMS_LAG + 2
        first_log_step = first_exp_step + GROUPS
        logs_per_step = 2
        log_steps = GROUPS // logs_per_step
        last_stage_lag = SUMS_LAG + 4
        for step in range(N_GROUPS + last_stage_lag):
            if 1 <= step <= N_GROUPS:
                quantise_group(step - 1)

            if step < N_GROUPS:
                transpose_group(step)
            ready = step - MULTIPLY_LAG
            if 0 <= ready < N_GROUPS and GATES[ready // GROUPS] != "c":
                multiply_group(ready, sum_psum, "sums")
            if step < N_GROUPS:
                empty_group(step)

            if step == 0:
                x_by_k = transpose_tokens(x_rows, "x")
            if step == MULTIPLY_LAG - 1:
                quantise_x()
            if step == SUMS_LAG - 1:
                deter_by_k = transpose_tokens(deter_rows, "deter")
                transpose_vectors()
            if step + LOADS_AHEAD < N_GROUPS:
                load_group(step + LOADS_AHEAD)

            when_due(step, "dt", SUMS_LAG, dt_argument)
            if step == first_exp_step:
                nc.scalar.activation(out=a_work[:], in_=a_work[:], func=ACT.Exp)
            one_a_step(step, first_exp_step, dt_exp)
            log_step = step - first_log_step
            if log_step == 0:
                nc.scalar.activation(out=a_work[:], in_=a_work[:], func=ACT.Ln, bias=one_col[:])
            if 0 <= log_step < log_steps:
                for j in range(logs_per_step * log_step, logs_per_step * (log_step + 1)):
                    dt_log(j)
            one_a_step(step, first_log_step + log_steps, decay_exp)
            when_due(step, "b", SUMS_LAG, b_tanh)
            when_due(step, "z", SUMS_LAG, z_tanh)
            when_due(step, "z", SUMS_LAG + 3, square)

            when_due(step, "z", SUMS_LAG + 2, add_deter)
            when_due(step, "z", SUMS_LAG + 1, gate_the_change)
            when_due(step, "b", SUMS_LAG + 4, y_minus_deter)
            when_due(step, "b", SUMS_LAG + 3, c_times_state)
            when_due(step, "b", SUMS_LAG + 2, new_state)
            when_due(step, "b", SUMS_LAG + 1, input_term)
            one_a_step(step, first_log_step + log_steps + 1, decay_times_deter)
            one_a_step(step, first_log_step + 2, dt_times_x)
            if log_step == 1:
                nc.vector.tensor_tensor(
                    out=a_work[:], in0=a_work[:], in1=columns_of(A_BASE), op=ALU.max
                )
                nc.vector.tensor_scalar_mul(out=a_neg[:], in0=a_work[:], scalar1=-1.0)
                nc.vector.tensor_scalar_mul(out=a_neg_dt_min[:], in0=a_work[:], scalar1=-DT_MIN)
            if 1 <= log_step <= log_steps:
                for j in range(logs_per_step * (log_step - 1), logs_per_step * log_step):
                    dt_softplus(j)
            one_a_step(step, SUMS_LAG, skip_minus_deter)
            when_due(step, "dt", SUMS_LAG + 1, dt_cap)

            when_due(step, "b", SUMS_LAG + 2, c_matmuls)
            when_due(step, "z", last_stage_lag, add_squares)

        nc.scalar.activation(out=sqrt_warm[:], in_=one_col[:], func=ACT.Sqrt)
        for j in range(GROUPS):
            for e in range(PAIR):
                cols = slice(TOKENS * e, TOKENS * (e + 1))
                nc.vector.tensor_scalar_mul(
                    out=mix[j][:, cols],
                    in0=mix[j][:, cols],
                    scalar1=channel_scalar(columns_of(NORM_W), j, e),
                )
        square_sum = const.tile([P, TOKEN_TILES], F32)
        by_token_tile = totals[0][:].rearrange("p (j t c) -> p t j c", t=TOKEN_TILES, c=ONES_COLS)
        nc.vector.tensor_reduce(
            out=square_sum[:],
            in_=by_token_tile[:, :, :, 0],
            axis=mybir.AxisListType.X,
            op=ALU.add,
        )
        rms = const.tile([P, TOKEN_TILES], F32)
        nc.scalar.activation(
            out=rms[:], in_=square_sum[:], func=ACT.Sqrt, bias=eps_col[:], scale=1.0 / CHANNELS
        )
        inv_rms = const.tile([P, TOKEN_TILES], F32)
        nc.vector.reciprocal(out=inv_rms[:], in_=rms[:])

        free_banks = (
            FLIP_BANKS * [(flip_psum, "flip")]
            + SUM_BANKS * [(sum_psum, "sums")]
            + LATE_BANKS * [(late_psum, "late")]
        )
        out_banks = []
        for first_group in range(0, GROUPS, GROUPS_PER_BANK):
            for t in range(TOKEN_TILES):
                pool, tag = free_banks[len(out_banks)]
                bank = pool.tile([P, BANK], F32, name="out_bank", tag=tag)
                for jj in range(GROUPS_PER_BANK):
                    for e in range(PAIR):
                        first = TOKENS * e + P * t
                        nc.tensor.transpose(
                            bank[:, P * (PAIR * jj + e) : P * (PAIR * jj + e + 1)],
                            mix[first_group + jj][:, first : first + P],
                            ident[:],
                        )
                out_banks.append((bank, first_group, t))
        for bank, first_group, t in out_banks:
            normed = store_pool.tile([P, BANK], F32, tag="normed")
            normed_view = normed[:].rearrange("p (j c e) -> p j c e", j=GROUPS_PER_BANK, e=PAIR)
            bank_view = bank[:].rearrange("p (j e c) -> p j c e", j=GROUPS_PER_BANK, e=PAIR)
            if t == 0:
                nc.scalar.activation(
                    out=normed_view, in_=bank_view, func=ACT.Copy, scale=inv_rms[:, t : t + 1]
                )
            else:
                nc.vector.tensor_scalar_mul(
                    out=normed_view, in0=bank_view, scalar1=inv_rms[:, t : t + 1]
                )
            first_channel = GROUP_ROWS * first_group
            nc.sync.dma_start(
                out=out[P * t : P * (t + 1), first_channel : first_channel + BANK], in_=normed[:]
            )
